import numpy as np
import ml_dtypes


def mxq(x, axis, fmt="e4m3"):
    dtype, down = {"e4m3": (ml_dtypes.float8_e4m3fn, 7), "e5m2": (ml_dtypes.float8_e5m2, 14)}[fmt]
    v = np.moveaxis(np.asarray(x, np.float32).astype(ml_dtypes.bfloat16).astype(np.float64), axis, -1)
    blocks = v.reshape(v.shape[:-1] + (-1, 32))
    amax = np.abs(blocks).max(-1, keepdims=True)
    byte = np.maximum(np.where(amax > 0, np.frexp(amax)[1] - 1 + 127, 0) - down, 1)
    scale = np.exp2(byte - 127.0)
    codes = (blocks / scale).astype(np.float32).astype(dtype).astype(np.float64)
    return np.moveaxis((codes * scale).reshape(v.shape), -1, axis)


WIDE = False


def mx_kscale(k):
    if not WIDE:
        return np.ones(k)
    levels = np.array([10, -10, 5, -5, 0])
    a = np.random.permutation(np.resize(levels, k // 512 * 4)).reshape(k // 512, 4)
    idx = np.arange(k)
    return np.exp2(a[idx // 512, idx % 128 // 32])


BF16 = ml_dtypes.bfloat16


def bf(x):
    return np.asarray(x, np.float32).astype(BF16)


def f64(x):
    return np.asarray(x).astype(np.float64)


B, T, E, H = 1, 1024, 512, 4
SW = np.sqrt(2.0) * (T / E) ** 0.25 / np.sqrt(E)


def setup_inputs():
    s = mx_kscale(E)
    return {"x": bf(np.random.standard_normal((B, T, E)) * s),
            "wq": bf(np.random.standard_normal((H, E, E)) * SW / s[:, None]),
            "wk": bf(np.random.standard_normal((H, E, E)) * SW / s[:, None])}


def reference(x, wq, wk):
    xq = mxq(f64(x)[None], 3, "e4m3")
    q = xq @ mxq(f64(wq)[:, None], 2, "e4m3")
    k = xq @ mxq(f64(wk)[:, None], 2, "e4m3")
    k_rs = k.reshape(H, B, E, T)
    return (mxq(q, 3, "e4m3") @ mxq(k_rs, 2, "e4m3")) / np.sqrt(T)

@@ -1,0 +1,205 @@
+from contextlib import ExitStack
+import math
+
+import concourse.mybir as mybir
+from concourse.masks import make_identity
+
+BF16 = mybir.dt.bfloat16
+F32 = mybir.dt.float32
+U32 = mybir.dt.uint32
+U8 = mybir.dt.uint8
+FP8X4 = mybir.dt.float8_e4m3fn_x4
+
+P = 128
+PACK = 4
+T, E, H = 1024, 512, 4
+BANK = 512
+CHUNKS = T // P
+W_CHUNKS = E // P
+UNITS = H * CHUNKS
+
+Q_AHEAD = 2
+K_AHEAD = CHUNKS + 2
+W_AHEAD = K_AHEAD + 2
+VECTOR_TURN = 4
+
+FLOPS = 2 * H * T * E * (2 * E + T)
+
+
+def chunk(i):
+    return slice(i * P, (i + 1) * P)
+
+
+def tile_multiheadattention_pa_kernel(tc, x, wq, wk, out):
+    nc = tc.nc
+    with ExitStack() as ctx:
+        keep = ctx.enter_context(tc.tile_pool(name="keep", bufs=1))
+        stage = ctx.enter_context(tc.tile_pool(name="stage", bufs=3))
+        results = ctx.enter_context(tc.tile_pool(name="results", bufs=4))
+        psum = ctx.enter_context(tc.psum_pool(name="psum", bufs=8))
+
+        x_rows = x[0].rearrange("(p r) e -> p r e", r=CHUNKS)
+        x_raw = []
+        for a in range(CHUNKS // 2):
+            piece = keep.tile([P, 2 * E], BF16, name="x_raw%d" % a)
+            nc.sync.dma_start(
+                out=piece[:].rearrange("p (r e) -> p r e", r=2),
+                in_=x_rows[:, 2 * a : 2 * a + 2, :],
+            )
+            x_raw.append(piece)
+
+        w_raw = []
+        for h in range(H):
+            for name, w in (("wk", wk), ("wq", wq)):
+                raw = keep.tile([P, PACK, E], BF16, name="%s_raw%d" % (name, h))
+                nc.sync.dma_start(
+                    out=raw[:].rearrange("p (u e) o -> p u e o", u=2),
+                    in_=w[h].rearrange("(u p e) o -> p u e o", u=2, e=2),
+                )
+                w_raw.append(raw)
+
+        identity = keep.tile([P, P], F32, name="identity")
+        make_identity(nc, identity[:])
+
+        warm = keep.tile([P, 1], F32, name="warm")
+        nc.vector.memset(warm[:], 0.0)
+        nc.scalar.mul(out=warm[:], in_=warm[:], mul=1.0)
+
+        def mx_operand(name, columns):
+            codes = keep.tile([P, columns], U32, name=name + "_codes", align_bytes=64)
+            scales = keep.tile([P, columns], U8, name=name + "_scales", align_bytes=64)
+            return codes, scales
+
+        def quantise(grouped, operand, columns):
+            codes, scales = operand
+            nc.vector.quantize_mx(
+                out=codes[:, columns].bitcast(FP8X4), scales=scales[:, columns], in_=grouped
+            )
+
+        def mx_product(acc, stationary, stationary_columns, moving, moving_columns):
+            nc.tensor.matmul_mx(
+                out=acc,
+                lhsT=stationary[0][:, stationary_columns].bitcast(FP8X4),
+                lhsT_scale=stationary[1][:, stationary_columns],
+                rhs=moving[0][:, moving_columns].bitcast(FP8X4),
+                rhs_scale=moving[1][:, moving_columns],
+                start=True,
+                stop=True,
+            )
+
+        x_mx = mx_operand("x", T)
+        w_mx = [mx_operand("w%d" % m, E) for m in range(2 * H)]
+        q_mx = [mx_operand("q%d" % h, T) for h in range(H)]
+        k_mx = [mx_operand("k%d" % h, T) for h in range(H)]
+
+        x_grouped = []
+        for a in range(CHUNKS // 2):
+            words = x_raw[a][:].bitcast(F32)
+            bank = psum.tile([P, 2, 2, P], F32, tag="bank", name="x_bank%d" % a)
+            for r in range(2):
+                for u in range(2):
+                    nc.tensor.transpose(bank[:, r, u, :], words[:, chunk(2 * r + u)], identity[:])
+            grouped = keep.tile([P, 2 * P * PACK], BF16, name="x_grouped%d" % a, align_bytes=64)
+            nc.scalar.copy(
+                out=grouped[:].bitcast(F32).rearrange("p (r t u) -> p r t u", r=2, u=2),
+                in_=bank[:].rearrange("p r u t -> p r t u"),
+            )
+            x_grouped.append(grouped)
+        for a in range(CHUNKS // 2):
+            quantise(x_grouped[a][:], x_mx, slice(2 * P * a, 2 * P * (a + 1)))
+
+        w_grouped = {}
+        q_grouped = {}
+        k_grouped = {}
+        result_of = {}
+
+        def regroup_weights(n):
+            matrix, c = divmod(n, W_CHUNKS)
+            raw = w_raw[matrix]
+            grouped = stage.tile(
+                [P, P * PACK], BF16, tag="w_grouped", name="w_grouped%d" % n, align_bytes=64
+            )
+            if matrix % 2 == 0:
+                nc.vector.tensor_copy(
+                    out=grouped[:].rearrange("p (n i t) -> p n t i", i=4, t=PACK),
+                    in_=raw[:, :, chunk(c)].rearrange("p t (n i) -> p n t i", i=4),
+                )
+            else:
+                nc.vector.tensor_copy(
+                    out=grouped[:].rearrange("p (m t) -> p m t", t=PACK),
+                    in_=raw[:].rearrange("p t (m c) -> p c m t", c=PACK)[:, c],
+                )
+            w_grouped[n] = grouped
+
+        def quantise_weights(n):
+            matrix, c = divmod(n, W_CHUNKS)
+            quantise(w_grouped[n][:], w_mx[matrix], chunk(c))
+
+        def empty_projection(bank, tag, n, copy_out):
+            grouped = stage.tile(
+                [P, P * PACK], BF16, tag=tag, name="%s%d" % (tag, n), align_bytes=64
+            )
+            copy_out(
+                out=grouped[:].rearrange("p (n c) -> p n c", c=PACK),
+                in_=bank[:].rearrange("p c n -> p n c"),
+            )
+            return grouped
+
+        def project_q(g, copy_out):
+            h, r = divmod(g, CHUNKS)
+            bank = psum.tile([P, PACK, P], F32, tag="bank", name="q_bank%d" % g)
+            for c in range(PACK):
+                mx_product(bank[:, c, :], w_mx[2 * h + 1], chunk(c), x_mx, chunk(r))
+            q_grouped[g] = empty_projection(bank, "q_grouped", g, copy_out)
+
+        def quantise_q(g):
+            h, r = divmod(g, CHUNKS)
+            quantise(q_grouped[g][:], q_mx[h], chunk(r))
+
+        def project_k(n, copy_out):
+            h, j_chunk = divmod(n, CHUNKS)
+            jh, b = divmod(j_chunk, W_CHUNKS)
+            bank = psum.tile([P, PACK, P], F32, tag="bank", name="k_bank%d" % n)
+            for c in range(PACK):
+                mx_product(bank[:, c, :], x_mx, chunk(2 * c + jh), w_mx[2 * h], chunk(b))
+            k_grouped[n] = empty_projection(bank, "k_grouped", n, copy_out)
+
+        def quantise_k(n):
+            h, j_chunk = divmod(n, CHUNKS)
+            quantise(k_grouped[n][:], k_mx[h], chunk(j_chunk))
+
+        out_rows = [out[h, 0].rearrange("(p r) j -> p r j", r=CHUNKS) for h in range(H)]
+
+        def scores(g):
+            h, r = divmod(g, CHUNKS)
+            if r % 2 == 0:
+                result_of[g // 2] = results.tile([P, 2, T], F32, tag="result", name="result%d" % g)
+            result = result_of[g // 2]
+            for jh in range(T // BANK):
+                columns = slice(jh * BANK, (jh + 1) * BANK)
+                bank = psum.tile([P, BANK], F32, tag="bank", name="s_bank%d_%d" % (g, jh))
+                mx_product(bank[:], q_mx[h], chunk(r), k_mx[h], columns)
+                nc.scalar.mul(out=result[:, r % 2, columns], in_=bank[:], mul=1.0 / math.sqrt(T))
+            if r % 2 == 1:
+                nc.sync.dma_start(out=out_rows[h][:, r - 1 : r + 1, :], in_=result[:])
+
+        for g in range(-W_AHEAD, UNITS):
+            filling = g < 0
+            if 0 <= g + Q_AHEAD < UNITS:
+                project_q(g + Q_AHEAD, nc.scalar.copy if filling else nc.vector.tensor_copy)
+            if 0 <= g + K_AHEAD < UNITS:
+                vector_turn = (g + K_AHEAD) % VECTOR_TURN == VECTOR_TURN - 1
+                project_k(
+                    g + K_AHEAD,
+                    nc.vector.tensor_copy if vector_turn and not filling else nc.scalar.copy,
+                )
+            if 0 <= g + Q_AHEAD - 1 < UNITS:
+                quantise_q(g + Q_AHEAD - 1)
+            if 0 <= g + K_AHEAD - 1 < UNITS:
+                quantise_k(g + K_AHEAD - 1)
+            if 0 <= g + W_AHEAD < UNITS:
+                regroup_weights(g + W_AHEAD)
+            if 0 <= g + W_AHEAD - 1 < UNITS:
+                quantise_weights(g + W_AHEAD - 1)
+            if g >= 0:
+                scores(g)

@@ -10,24 +10,26 @@ U32 = mybir.dt.uint32
 U8 = mybir.dt.uint8
 FP8X4 = mybir.dt.float8_e4m3fn_x4
 
+COPY = mybir.ActivationFunctionType.Copy
+
 P = 128
 PACK = 4
 T, E, H = 1024, 512, 4
 BANK = 512
 CHUNKS = T // P
-W_CHUNKS = E // P
 UNITS = H * CHUNKS
+GROUP = P * PACK
 
-Q_AHEAD = 2
-K_AHEAD = CHUNKS + 2
-W_AHEAD = K_AHEAD + 2
+Q_AHEAD = 4
+K_AHEAD = CHUNKS + 4
+W_AHEAD = K_AHEAD + 3
 VECTOR_TURN = 4
 
 FLOPS = 2 * H * T * E * (2 * E + T)
 
 
-def chunk(i):
-    return slice(i * P, (i + 1) * P)
+def columns(i, width):
+    return slice(i * width, (i + 1) * width)
 
 
 def tile_multiheadattention_pa_kernel(tc, x, wq, wk, out):
@@ -37,7 +39,17 @@ def tile_multiheadattention_pa_kernel(tc, x, wq, wk, out):
         stage = ctx.enter_context(tc.tile_pool(name="stage", bufs=3))
         results = ctx.enter_context(tc.tile_pool(name="results", bufs=4))
         psum = ctx.enter_context(tc.psum_pool(name="psum", bufs=8))
+        ctx.enter_context(tc.manual_schedule())
 
+        def load_weights(w, h, name):
+            raw = keep.tile([P, PACK, E], BF16, name="%s_raw%d" % (name, h))
+            nc.sync.dma_start(
+                out=raw[:].rearrange("p (u e) o -> p u e o", u=2),
+                in_=w[h].rearrange("(u p e) o -> p u e o", u=2, e=2),
+            )
+            return raw
+
+        w_raw = [load_weights(wk, 0, "wk")]
         x_rows = x[0].rearrange("(p r) e -> p r e", r=CHUNKS)
         x_raw = []
         for a in range(CHUNKS // 2):
@@ -47,33 +59,27 @@ def tile_multiheadattention_pa_kernel(tc, x, wq, wk, out):
                 in_=x_rows[:, 2 * a : 2 * a + 2, :],
             )
             x_raw.append(piece)
-
-        w_raw = []
-        for h in range(H):
-            for name, w in (("wk", wk), ("wq", wq)):
-                raw = keep.tile([P, PACK, E], BF16, name="%s_raw%d" % (name, h))
-                nc.sync.dma_start(
-                    out=raw[:].rearrange("p (u e) o -> p u e o", u=2),
-                    in_=w[h].rearrange("(u p e) o -> p u e o", u=2, e=2),
-                )
-                w_raw.append(raw)
+        w_raw.append(load_weights(wq, 0, "wq"))
+        for h in range(1, H):
+            w_raw.append(load_weights(wk, h, "wk"))
+            w_raw.append(load_weights(wq, h, "wq"))
 
         identity = keep.tile([P, P], F32, name="identity")
         make_identity(nc, identity[:])
 
         warm = keep.tile([P, 1], F32, name="warm")
         nc.vector.memset(warm[:], 0.0)
-        nc.scalar.mul(out=warm[:], in_=warm[:], mul=1.0)
+        nc.scalar.activation(out=warm[:], in_=warm[:], func=COPY)
 
-        def mx_operand(name, columns):
-            codes = keep.tile([P, columns], U32, name=name + "_codes", align_bytes=64)
-            scales = keep.tile([P, columns], U8, name=name + "_scales", align_bytes=64)
+        def mx_operand(name, width):
+            codes = keep.tile([P, width], U32, name=name + "_codes", align_bytes=64)
+            scales = keep.tile([P, width], U8, name=name + "_scales", align_bytes=64)
             return codes, scales
 
-        def quantise(grouped, operand, columns):
+        def quantise(grouped, operand, where):
             codes, scales = operand
             nc.vector.quantize_mx(
-                out=codes[:, columns].bitcast(FP8X4), scales=scales[:, columns], in_=grouped
+                out=codes[:, where].bitcast(FP8X4), scales=scales[:, where], in_=grouped[:]
             )
 
         def mx_product(acc, stationary, stationary_columns, moving, moving_columns):
@@ -92,114 +98,162 @@ def tile_multiheadattention_pa_kernel(tc, x, wq, wk, out):
         q_mx = [mx_operand("q%d" % h, T) for h in range(H)]
         k_mx = [mx_operand("k%d" % h, T) for h in range(H)]
 
-        x_grouped = []
-        for a in range(CHUNKS // 2):
-            words = x_raw[a][:].bitcast(F32)
-            bank = psum.tile([P, 2, 2, P], F32, tag="bank", name="x_bank%d" % a)
-            for r in range(2):
-                for u in range(2):
-                    nc.tensor.transpose(bank[:, r, u, :], words[:, chunk(2 * r + u)], identity[:])
-            grouped = keep.tile([P, 2 * P * PACK], BF16, name="x_grouped%d" % a, align_bytes=64)
-            nc.scalar.copy(
-                out=grouped[:].bitcast(F32).rearrange("p (r t u) -> p r t u", r=2, u=2),
-                in_=bank[:].rearrange("p r u t -> p r t u"),
-            )
-            x_grouped.append(grouped)
-        for a in range(CHUNKS // 2):
-            quantise(x_grouped[a][:], x_mx, slice(2 * P * a, 2 * P * (a + 1)))
+        def prepare_x():
+            x_grouped = []
+            for a in range(CHUNKS // 2):
+                words = x_raw[a][:].bitcast(F32)
+                bank = psum.tile([P, 2, 2, P], F32, tag="bank", name="x_bank%d" % a)
+                for r in range(2):
+                    for u in range(2):
+                        nc.tensor.transpose(
+                            bank[:, r, u, :], words[:, columns(2 * r + u, P)], identity[:]
+                        )
+                grouped = keep.tile([P, 2 * GROUP], BF16, name="x_grouped%d" % a, align_bytes=64)
+                nc.scalar.copy(
+                    out=grouped[:].bitcast(F32).rearrange("p (r t u) -> p r t u", r=2, u=2),
+                    in_=bank[:].rearrange("p r u t -> p r t u"),
+                )
+                x_grouped.append(grouped)
+            for a in range(CHUNKS // 2):
+                quantise(x_grouped[a], x_mx, columns(a, 2 * P))
 
         w_grouped = {}
-        q_grouped = {}
-        k_grouped = {}
-        result_of = {}
+        q_bank, q_grouped = {}, {}
+        k_bank, k_grouped = {}, {}
+        s_bank, result_of = {}, {}
 
         def regroup_weights(n):
-            matrix, c = divmod(n, W_CHUNKS)
+            matrix, half = divmod(n, 2)
             raw = w_raw[matrix]
             grouped = stage.tile(
-                [P, P * PACK], BF16, tag="w_grouped", name="w_grouped%d" % n, align_bytes=64
+                [P, 2 * GROUP], BF16, tag="w_grouped", name="w_grouped%d" % n, align_bytes=64
             )
             if matrix % 2 == 0:
                 nc.vector.tensor_copy(
                     out=grouped[:].rearrange("p (n i t) -> p n t i", i=4, t=PACK),
-                    in_=raw[:, :, chunk(c)].rearrange("p t (n i) -> p n t i", i=4),
+                    in_=raw[:, :, columns(half, 2 * P)].rearrange("p t (n i) -> p n t i", i=4),
                 )
             else:
                 nc.vector.tensor_copy(
-                    out=grouped[:].rearrange("p (m t) -> p m t", t=PACK),
-                    in_=raw[:].rearrange("p t (m c) -> p c m t", c=PACK)[:, c],
+                    out=grouped[:].rearrange("p (c m t) -> p c m t", c=2, t=PACK),
+                    in_=raw[:].rearrange("p t (m c) -> p c m t", c=PACK)[:, 2 * half : 2 * half + 2],
                 )
             w_grouped[n] = grouped
 
         def quantise_weights(n):
-            matrix, c = divmod(n, W_CHUNKS)
-            quantise(w_grouped[n][:], w_mx[matrix], chunk(c))
+            matrix, half = divmod(n, 2)
+            quantise(w_grouped[n], w_mx[matrix], columns(half, 2 * P))
 
-        def empty_projection(bank, tag, n, copy_out):
-            grouped = stage.tile(
-                [P, P * PACK], BF16, tag=tag, name="%s%d" % (tag, n), align_bytes=64
-            )
+        def empty_projection(copy_out, bank, grouped, place):
             copy_out(
-                out=grouped[:].rearrange("p (n c) -> p n c", c=PACK),
+                out=grouped[:, columns(place, GROUP)].rearrange("p (n c) -> p n c", c=PACK),
                 in_=bank[:].rearrange("p c n -> p n c"),
             )
-            return grouped
 
-        def project_q(g, copy_out):
+        def project_q(g):
             h, r = divmod(g, CHUNKS)
             bank = psum.tile([P, PACK, P], F32, tag="bank", name="q_bank%d" % g)
             for c in range(PACK):
-                mx_product(bank[:, c, :], w_mx[2 * h + 1], chunk(c), x_mx, chunk(r))
-            q_grouped[g] = empty_projection(bank, "q_grouped", g, copy_out)
+                mx_product(bank[:, c, :], w_mx[2 * h + 1], columns(c, P), x_mx, columns(r, P))
+            q_bank[g] = bank
 
-        def quantise_q(g):
+        def empty_q_pair(g, copy_out):
+            grouped = stage.tile(
+                [P, 2 * GROUP], BF16, tag="q_grouped", name="q_grouped%d" % g, align_bytes=64
+            )
+            empty_projection(copy_out, q_bank[g + 1], grouped, 1)
+            empty_projection(copy_out, q_bank[g], grouped, 0)
+            q_grouped[g] = grouped
+
+        def quantise_q_pair(g):
             h, r = divmod(g, CHUNKS)
-            quantise(q_grouped[g][:], q_mx[h], chunk(r))
+            quantise(q_grouped[g], q_mx[h], columns(r // 2, 2 * P))
 
-        def project_k(n, copy_out):
+        def project_k(n):
             h, j_chunk = divmod(n, CHUNKS)
-            jh, b = divmod(j_chunk, W_CHUNKS)
+            jh, b = divmod(j_chunk, PACK)
             bank = psum.tile([P, PACK, P], F32, tag="bank", name="k_bank%d" % n)
             for c in range(PACK):
-                mx_product(bank[:, c, :], x_mx, chunk(2 * c + jh), w_mx[2 * h], chunk(b))
-            k_grouped[n] = empty_projection(bank, "k_grouped", n, copy_out)
+                mx_product(bank[:, c, :], x_mx, columns(2 * c + jh, P), w_mx[2 * h], columns(b, P))
+            k_bank[n] = bank
 
-        def quantise_k(n):
-            h, j_chunk = divmod(n, CHUNKS)
-            quantise(k_grouped[n][:], k_mx[h], chunk(j_chunk))
+        def empty_k(n, copy_out):
+            if n % PACK == 0:
+                k_grouped[n // PACK] = stage.tile(
+                    [P, PACK * GROUP], BF16, tag="k_grouped", name="k_grouped%d" % n, align_bytes=64
+                )
+            empty_projection(copy_out, k_bank[n], k_grouped[n // PACK], n % PACK)
+
+        def quantise_k(half):
+            quantise(k_grouped[half], k_mx[half // 2], columns(half % 2, BANK))
+
+        def multiply_scores(g):
+            h, r = divmod(g, CHUNKS)
+            for jh in range(T // BANK):
+                bank = psum.tile([P, BANK], F32, tag="bank", name="s_bank%d_%d" % (g, jh))
+                mx_product(bank[:], q_mx[h], columns(r, P), k_mx[h], columns(jh, BANK))
+                s_bank[(g, jh)] = bank
+
+        def empty_scores(g, jh):
+            nc.scalar.activation(
+                out=result_of[g // 2][:, g % 2, columns(jh, BANK)],
+                in_=s_bank[(g, jh)][:],
+                func=COPY,
+                scale=1.0 / math.sqrt(T),
+            )
 
         out_rows = [out[h, 0].rearrange("(p r) j -> p r j", r=CHUNKS) for h in range(H)]
 
-        def scores(g):
+        def store_pair(g):
             h, r = divmod(g, CHUNKS)
-            if r % 2 == 0:
-                result_of[g // 2] = results.tile([P, 2, T], F32, tag="result", name="result%d" % g)
-            result = result_of[g // 2]
-            for jh in range(T // BANK):
-                columns = slice(jh * BANK, (jh + 1) * BANK)
-                bank = psum.tile([P, BANK], F32, tag="bank", name="s_bank%d_%d" % (g, jh))
-                mx_product(bank[:], q_mx[h], chunk(r), k_mx[h], columns)
-                nc.scalar.mul(out=result[:, r % 2, columns], in_=bank[:], mul=1.0 / math.sqrt(T))
-            if r % 2 == 1:
-                nc.sync.dma_start(out=out_rows[h][:, r - 1 : r + 1, :], in_=result[:])
+            nc.sync.dma_start(out=out_rows[h][:, r - 1 : r + 1, :], in_=result_of[g // 2][:])
+
+        def exists(i):
+            return 0 <= i < UNITS
+
+        def vector_empties_k(n, g):
+            return g >= 0 and n % VECTOR_TURN == 0
 
         for g in range(-W_AHEAD, UNITS):
-            filling = g < 0
-            if 0 <= g + Q_AHEAD < UNITS:
-                project_q(g + Q_AHEAD, nc.scalar.copy if filling else nc.vector.tensor_copy)
-            if 0 <= g + K_AHEAD < UNITS:
-                vector_turn = (g + K_AHEAD) % VECTOR_TURN == VECTOR_TURN - 1
-                project_k(
-                    g + K_AHEAD,
-                    nc.vector.tensor_copy if vector_turn and not filling else nc.scalar.copy,
-                )
-            if 0 <= g + Q_AHEAD - 1 < UNITS:
-                quantise_q(g + Q_AHEAD - 1)
-            if 0 <= g + K_AHEAD - 1 < UNITS:
-                quantise_k(g + K_AHEAD - 1)
-            if 0 <= g + W_AHEAD < UNITS:
-                regroup_weights(g + W_AHEAD)
-            if 0 <= g + W_AHEAD - 1 < UNITS:
-                quantise_weights(g + W_AHEAD - 1)
+            even = g % 2 == 0
+            new_k = g + K_AHEAD
+            new_q = g + Q_AHEAD
+            if new_k == 0:
+                prepare_x()
+
             if g >= 0:
-                scores(g)
+                multiply_scores(g)
+            if exists(new_k):
+                project_k(new_k)
+            if even and exists(new_q):
+                project_q(new_q)
+                project_q(new_q + 1)
+
+            if g >= 0:
+                if even:
+                    result_of[g // 2] = results.tile([P, 2, T], F32, tag="result", name="result%d" % g)
+                empty_scores(g, 1)
+            if even and g < 0 and exists(new_q):
+                empty_q_pair(new_q, nc.scalar.copy)
+            if exists(new_k - 1) and not vector_empties_k(new_k - 1, g - 1):
+                empty_k(new_k - 1, nc.scalar.copy)
+            if g >= 0:
+                empty_scores(g, 0)
+                if not even:
+                    store_pair(g)
+
+            if even:
+                if g >= 0 and exists(new_q):
+                    empty_q_pair(new_q, nc.vector.tensor_copy)
+                if exists(new_k) and vector_empties_k(new_k, g):
+                    empty_k(new_k, nc.vector.tensor_copy)
+            else:
+                new_w = (g + W_AHEAD) // 2
+                if exists(2 * (new_w - 1)):
+                    quantise_weights(new_w - 1)
+                if exists(2 * new_w):
+                    regroup_weights(new_w)
+                if exists(new_k - 2) and (new_k - 2) % PACK == PACK - 1:
+                    quantise_k((new_k - 2) // PACK)
+                if exists(new_q - 1):
+                    quantise_q_pair(new_q - 1)

@@ -11,6 +11,8 @@ U8 = mybir.dt.uint8
 FP8X4 = mybir.dt.float8_e4m3fn_x4
 
 COPY = mybir.ActivationFunctionType.Copy
+MULT = mybir.AluOpType.mult
+ADD = mybir.AluOpType.add
 
 P = 128
 PACK = 4
@@ -23,7 +25,7 @@ GROUP = P * PACK
 Q_AHEAD = 4
 K_AHEAD = CHUNKS + 4
 W_AHEAD = K_AHEAD + 3
-VECTOR_TURN = 4
+VECTOR_TURN = 2
 
 FLOPS = 2 * H * T * E * (2 * E + T)
 
@@ -37,6 +39,7 @@ def tile_multiheadattention_pa_kernel(tc, x, wq, wk, out):
     with ExitStack() as ctx:
         keep = ctx.enter_context(tc.tile_pool(name="keep", bufs=1))
         stage = ctx.enter_context(tc.tile_pool(name="stage", bufs=3))
+        weights_stage = ctx.enter_context(tc.tile_pool(name="weights_stage", bufs=1))
         results = ctx.enter_context(tc.tile_pool(name="results", bufs=4))
         psum = ctx.enter_context(tc.psum_pool(name="psum", bufs=8))
         ctx.enter_context(tc.manual_schedule())
@@ -50,15 +53,16 @@ def tile_multiheadattention_pa_kernel(tc, x, wq, wk, out):
             return raw
 
         w_raw = [load_weights(wk, 0, "wk")]
-        x_rows = x[0].rearrange("(p r) e -> p r e", r=CHUNKS)
+        x_chunks = x[0].rearrange("(p c jh) e -> p jh c e", c=PACK, jh=2)
         x_raw = []
-        for a in range(CHUNKS // 2):
-            piece = keep.tile([P, 2 * E], BF16, name="x_raw%d" % a)
-            nc.sync.dma_start(
-                out=piece[:].rearrange("p (r e) -> p r e", r=2),
-                in_=x_rows[:, 2 * a : 2 * a + 2, :],
-            )
-            x_raw.append(piece)
+        for jh in range(2):
+            for c in range(0, PACK, 2):
+                piece = keep.tile([P, 2 * E], BF16, name="x_raw%d" % len(x_raw))
+                nc.sync.dma_start(
+                    out=piece[:].rearrange("p (c e) -> p c e", c=2),
+                    in_=x_chunks[:, jh, c : c + 2, :],
+                )
+                x_raw.append(piece)
         w_raw.append(load_weights(wq, 0, "wq"))
         for h in range(1, H):
             w_raw.append(load_weights(wk, h, "wk"))
@@ -98,9 +102,12 @@ def tile_multiheadattention_pa_kernel(tc, x, wq, wk, out):
         q_mx = [mx_operand("q%d" % h, T) for h in range(H)]
         k_mx = [mx_operand("k%d" % h, T) for h in range(H)]
 
-        def prepare_x():
-            x_grouped = []
-            for a in range(CHUNKS // 2):
+        def x_place(r):
+            return columns(PACK * (r % 2) + r // 2, P)
+
+        def prepare_x(jh):
+            x_grouped = {}
+            for a in (2 * jh, 2 * jh + 1):
                 words = x_raw[a][:].bitcast(F32)
                 bank = psum.tile([P, 2, 2, P], F32, tag="bank", name="x_bank%d" % a)
                 for r in range(2):
@@ -113,8 +120,8 @@ def tile_multiheadattention_pa_kernel(tc, x, wq, wk, out):
                     out=grouped[:].bitcast(F32).rearrange("p (r t u) -> p r t u", r=2, u=2),
                     in_=bank[:].rearrange("p r u t -> p r t u"),
                 )
-                x_grouped.append(grouped)
-            for a in range(CHUNKS // 2):
+                x_grouped[a] = grouped
+            for a in (2 * jh, 2 * jh + 1):
                 quantise(x_grouped[a], x_mx, columns(a, 2 * P))
 
         w_grouped = {}
@@ -122,19 +129,22 @@ def tile_multiheadattention_pa_kernel(tc, x, wq, wk, out):
         k_bank, k_grouped = {}, {}
         s_bank, result_of = {}, {}
 
-        def regroup_weights(n):
+        def gpsimd_copy(out, in_):
+            nc.gpsimd.tensor_scalar(out=out, in0=in_, scalar1=1.0, scalar2=0.0, op0=MULT, op1=ADD)
+
+        def regroup_weights(n, copy):
             matrix, half = divmod(n, 2)
             raw = w_raw[matrix]
-            grouped = stage.tile(
+            grouped = weights_stage.tile(
                 [P, 2 * GROUP], BF16, tag="w_grouped", name="w_grouped%d" % n, align_bytes=64
             )
             if matrix % 2 == 0:
-                nc.vector.tensor_copy(
-                    out=grouped[:].rearrange("p (n i t) -> p n t i", i=4, t=PACK),
-                    in_=raw[:, :, columns(half, 2 * P)].rearrange("p t (n i) -> p n t i", i=4),
+                copy(
+                    out=grouped[:].rearrange("p (o t) -> p o t", t=PACK),
+                    in_=raw[:, :, columns(half, 2 * P)].rearrange("p t o -> p o t"),
                 )
             else:
-                nc.vector.tensor_copy(
+                copy(
                     out=grouped[:].rearrange("p (c m t) -> p c m t", c=2, t=PACK),
                     in_=raw[:].rearrange("p t (m c) -> p c m t", c=PACK)[:, 2 * half : 2 * half + 2],
                 )
@@ -154,7 +164,7 @@ def tile_multiheadattention_pa_kernel(tc, x, wq, wk, out):
             h, r = divmod(g, CHUNKS)
             bank = psum.tile([P, PACK, P], F32, tag="bank", name="q_bank%d" % g)
             for c in range(PACK):
-                mx_product(bank[:, c, :], w_mx[2 * h + 1], columns(c, P), x_mx, columns(r, P))
+                mx_product(bank[:, c, :], w_mx[2 * h + 1], columns(c, P), x_mx, x_place(r))
             q_bank[g] = bank
 
         def empty_q_pair(g, copy_out):
@@ -174,7 +184,7 @@ def tile_multiheadattention_pa_kernel(tc, x, wq, wk, out):
             jh, b = divmod(j_chunk, PACK)
             bank = psum.tile([P, PACK, P], F32, tag="bank", name="k_bank%d" % n)
             for c in range(PACK):
-                mx_product(bank[:, c, :], x_mx, columns(2 * c + jh, P), w_mx[2 * h], columns(b, P))
+                mx_product(bank[:, c, :], x_mx, x_place(2 * c + jh), w_mx[2 * h], columns(b, P))
             k_bank[n] = bank
 
         def empty_k(n, copy_out):
@@ -208,6 +218,13 @@ def tile_multiheadattention_pa_kernel(tc, x, wq, wk, out):
             h, r = divmod(g, CHUNKS)
             nc.sync.dma_start(out=out_rows[h][:, r - 1 : r + 1, :], in_=result_of[g // 2][:])
 
+        def store_bank(g, jh):
+            h, r = divmod(g, CHUNKS)
+            nc.sync.dma_start(
+                out=out_rows[h][:, r, columns(jh, BANK)],
+                in_=result_of[g // 2][:, g % 2, columns(jh, BANK)],
+            )
+
         def exists(i):
             return 0 <= i < UNITS
 
@@ -218,8 +235,9 @@ def tile_multiheadattention_pa_kernel(tc, x, wq, wk, out):
             even = g % 2 == 0
             new_k = g + K_AHEAD
             new_q = g + Q_AHEAD
-            if new_k == 0:
-                prepare_x()
+            last_pair = g // 2 == UNITS // 2 - 1
+            if new_k == 0 or new_k == PACK:
+                prepare_x(new_k // PACK)
 
             if g >= 0:
                 multiply_scores(g)
@@ -233,13 +251,17 @@ def tile_multiheadattention_pa_kernel(tc, x, wq, wk, out):
                 if even:
                     result_of[g // 2] = results.tile([P, 2, T], F32, tag="result", name="result%d" % g)
                 empty_scores(g, 1)
+                if last_pair:
+                    store_bank(g, 1)
             if even and g < 0 and exists(new_q):
                 empty_q_pair(new_q, nc.scalar.copy)
             if exists(new_k - 1) and not vector_empties_k(new_k - 1, g - 1):
                 empty_k(new_k - 1, nc.scalar.copy)
             if g >= 0:
                 empty_scores(g, 0)
-                if not even:
+                if last_pair:
+                    store_bank(g, 0)
+                elif not even:
                     store_pair(g)
 
             if even:
@@ -249,11 +271,11 @@ def tile_multiheadattention_pa_kernel(tc, x, wq, wk, out):
                     empty_k(new_k, nc.vector.tensor_copy)
             else:
                 new_w = (g + W_AHEAD) // 2
-                if exists(2 * (new_w - 1)):
-                    quantise_weights(new_w - 1)
-                if exists(2 * new_w):
-                    regroup_weights(new_w)
                 if exists(new_k - 2) and (new_k - 2) % PACK == PACK - 1:
                     quantise_k((new_k - 2) // PACK)
                 if exists(new_q - 1):
                     quantise_q_pair(new_q - 1)
+                if exists(2 * (new_w - 1)):
+                    quantise_weights(new_w - 1)
+                if exists(2 * new_w):
+                    regroup_weights(new_w, nc.vector.tensor_copy if g < 0 else gpsimd_copy)

@@ -11,8 +11,6 @@ U8 = mybir.dt.uint8
 FP8X4 = mybir.dt.float8_e4m3fn_x4
 
 COPY = mybir.ActivationFunctionType.Copy
-MULT = mybir.AluOpType.mult
-ADD = mybir.AluOpType.add
 
 P = 128
 PACK = 4
@@ -25,7 +23,9 @@ GROUP = P * PACK
 Q_AHEAD = 4
 K_AHEAD = CHUNKS + 4
 W_AHEAD = K_AHEAD + 3
-VECTOR_TURN = 2
+VECTOR_TURN = 4
+
+SCALE = 1.0 / math.sqrt(T)
 
 FLOPS = 2 * H * T * E * (2 * E + T)
 
@@ -39,8 +39,7 @@ def tile_multiheadattention_pa_kernel(tc, x, wq, wk, out):
     with ExitStack() as ctx:
         keep = ctx.enter_context(tc.tile_pool(name="keep", bufs=1))
         stage = ctx.enter_context(tc.tile_pool(name="stage", bufs=3))
-        weights_stage = ctx.enter_context(tc.tile_pool(name="weights_stage", bufs=1))
-        results = ctx.enter_context(tc.tile_pool(name="results", bufs=4))
+        results = ctx.enter_context(tc.tile_pool(name="results", bufs=8))
         psum = ctx.enter_context(tc.psum_pool(name="psum", bufs=8))
         ctx.enter_context(tc.manual_schedule())
 
@@ -53,16 +52,15 @@ def tile_multiheadattention_pa_kernel(tc, x, wq, wk, out):
             return raw
 
         w_raw = [load_weights(wk, 0, "wk")]
-        x_chunks = x[0].rearrange("(p c jh) e -> p jh c e", c=PACK, jh=2)
+        x_rows = x[0].rearrange("(p r) e -> p r e", r=CHUNKS)
         x_raw = []
-        for jh in range(2):
-            for c in range(0, PACK, 2):
-                piece = keep.tile([P, 2 * E], BF16, name="x_raw%d" % len(x_raw))
-                nc.sync.dma_start(
-                    out=piece[:].rearrange("p (c e) -> p c e", c=2),
-                    in_=x_chunks[:, jh, c : c + 2, :],
-                )
-                x_raw.append(piece)
+        for a in range(CHUNKS // 2):
+            piece = keep.tile([P, 2 * E], BF16, name="x_raw%d" % a)
+            nc.sync.dma_start(
+                out=piece[:].rearrange("p (r e) -> p r e", r=2),
+                in_=x_rows[:, 2 * a : 2 * a + 2, :],
+            )
+            x_raw.append(piece)
         w_raw.append(load_weights(wq, 0, "wq"))
         for h in range(1, H):
             w_raw.append(load_weights(wk, h, "wk"))
@@ -102,12 +100,9 @@ def tile_multiheadattention_pa_kernel(tc, x, wq, wk, out):
         q_mx = [mx_operand("q%d" % h, T) for h in range(H)]
         k_mx = [mx_operand("k%d" % h, T) for h in range(H)]
 
-        def x_place(r):
-            return columns(PACK * (r % 2) + r // 2, P)
-
-        def prepare_x(jh):
-            x_grouped = {}
-            for a in (2 * jh, 2 * jh + 1):
+        def prepare_x():
+            x_grouped = []
+            for a in range(CHUNKS // 2):
                 words = x_raw[a][:].bitcast(F32)
                 bank = psum.tile([P, 2, 2, P], F32, tag="bank", name="x_bank%d" % a)
                 for r in range(2):
@@ -120,8 +115,8 @@ def tile_multiheadattention_pa_kernel(tc, x, wq, wk, out):
                     out=grouped[:].bitcast(F32).rearrange("p (r t u) -> p r t u", r=2, u=2),
                     in_=bank[:].rearrange("p r u t -> p r t u"),
                 )
-                x_grouped[a] = grouped
-            for a in (2 * jh, 2 * jh + 1):
+                x_grouped.append(grouped)
+            for a in range(CHUNKS // 2):
                 quantise(x_grouped[a], x_mx, columns(a, 2 * P))
 
         w_grouped = {}
@@ -129,22 +124,19 @@ def tile_multiheadattention_pa_kernel(tc, x, wq, wk, out):
         k_bank, k_grouped = {}, {}
         s_bank, result_of = {}, {}
 
-        def gpsimd_copy(out, in_):
-            nc.gpsimd.tensor_scalar(out=out, in0=in_, scalar1=1.0, scalar2=0.0, op0=MULT, op1=ADD)
-
-        def regroup_weights(n, copy):
+        def regroup_weights(n):
             matrix, half = divmod(n, 2)
             raw = w_raw[matrix]
-            grouped = weights_stage.tile(
+            grouped = stage.tile(
                 [P, 2 * GROUP], BF16, tag="w_grouped", name="w_grouped%d" % n, align_bytes=64
             )
             if matrix % 2 == 0:
-                copy(
-                    out=grouped[:].rearrange("p (o t) -> p o t", t=PACK),
-                    in_=raw[:, :, columns(half, 2 * P)].rearrange("p t o -> p o t"),
+                nc.vector.tensor_copy(
+                    out=grouped[:].rearrange("p (n i t) -> p n t i", i=4, t=PACK),
+                    in_=raw[:, :, columns(half, 2 * P)].rearrange("p t (n i) -> p n t i", i=4),
                 )
             else:
-                copy(
+                nc.vector.tensor_copy(
                     out=grouped[:].rearrange("p (c m t) -> p c m t", c=2, t=PACK),
                     in_=raw[:].rearrange("p t (m c) -> p c m t", c=PACK)[:, 2 * half : 2 * half + 2],
                 )
@@ -164,7 +156,7 @@ def tile_multiheadattention_pa_kernel(tc, x, wq, wk, out):
             h, r = divmod(g, CHUNKS)
             bank = psum.tile([P, PACK, P], F32, tag="bank", name="q_bank%d" % g)
             for c in range(PACK):
-                mx_product(bank[:, c, :], w_mx[2 * h + 1], columns(c, P), x_mx, x_place(r))
+                mx_product(bank[:, c, :], w_mx[2 * h + 1], columns(c, P), x_mx, columns(r, P))
             q_bank[g] = bank
 
         def empty_q_pair(g, copy_out):
@@ -184,7 +176,7 @@ def tile_multiheadattention_pa_kernel(tc, x, wq, wk, out):
             jh, b = divmod(j_chunk, PACK)
             bank = psum.tile([P, PACK, P], F32, tag="bank", name="k_bank%d" % n)
             for c in range(PACK):
-                mx_product(bank[:, c, :], x_mx, x_place(2 * c + jh), w_mx[2 * h], columns(b, P))
+                mx_product(bank[:, c, :], x_mx, columns(2 * c + jh, P), w_mx[2 * h], columns(b, P))
             k_bank[n] = bank
 
         def empty_k(n, copy_out):
@@ -204,26 +196,18 @@ def tile_multiheadattention_pa_kernel(tc, x, wq, wk, out):
                 mx_product(bank[:], q_mx[h], columns(r, P), k_mx[h], columns(jh, BANK))
                 s_bank[(g, jh)] = bank
 
-        def empty_scores(g, jh):
-            nc.scalar.activation(
-                out=result_of[g // 2][:, g % 2, columns(jh, BANK)],
-                in_=s_bank[(g, jh)][:],
-                func=COPY,
-                scale=1.0 / math.sqrt(T),
-            )
+        def empty_scores(g, jh, on_vector):
+            half_rows = result_of[g][:, columns(jh, BANK)]
+            if on_vector:
+                nc.vector.tensor_scalar_mul(out=half_rows, in0=s_bank[(g, jh)][:], scalar1=SCALE)
+            else:
+                nc.scalar.activation(out=half_rows, in_=s_bank[(g, jh)][:], func=COPY, scale=SCALE)
 
         out_rows = [out[h, 0].rearrange("(p r) j -> p r j", r=CHUNKS) for h in range(H)]
 
-        def store_pair(g):
+        def store_unit(g):
             h, r = divmod(g, CHUNKS)
-            nc.sync.dma_start(out=out_rows[h][:, r - 1 : r + 1, :], in_=result_of[g // 2][:])
-
-        def store_bank(g, jh):
-            h, r = divmod(g, CHUNKS)
-            nc.sync.dma_start(
-                out=out_rows[h][:, r, columns(jh, BANK)],
-                in_=result_of[g // 2][:, g % 2, columns(jh, BANK)],
-            )
+            nc.sync.dma_start(out=out_rows[h][:, r, :], in_=result_of[g][:])
 
         def exists(i):
             return 0 <= i < UNITS
@@ -235,9 +219,10 @@ def tile_multiheadattention_pa_kernel(tc, x, wq, wk, out):
             even = g % 2 == 0
             new_k = g + K_AHEAD
             new_q = g + Q_AHEAD
-            last_pair = g // 2 == UNITS // 2 - 1
-            if new_k == 0 or new_k == PACK:
-                prepare_x(new_k // PACK)
+            new_w = (g + W_AHEAD) // 2
+            vector_helps = g >= 0 and not even and not exists(2 * new_w)
+            if new_k == 0:
+                prepare_x()
 
             if g >= 0:
                 multiply_scores(g)
@@ -248,34 +233,31 @@ def tile_multiheadattention_pa_kernel(tc, x, wq, wk, out):
                 project_q(new_q + 1)
 
             if g >= 0:
-                if even:
-                    result_of[g // 2] = results.tile([P, 2, T], F32, tag="result", name="result%d" % g)
-                empty_scores(g, 1)
-                if last_pair:
-                    store_bank(g, 1)
-            if even and g < 0 and exists(new_q):
-                empty_q_pair(new_q, nc.scalar.copy)
+                result_of[g] = results.tile([P, T], F32, tag="result", name="result%d" % g)
+                empty_scores(g, 1, on_vector=False)
             if exists(new_k - 1) and not vector_empties_k(new_k - 1, g - 1):
                 empty_k(new_k - 1, nc.scalar.copy)
-            if g >= 0:
-                empty_scores(g, 0)
-                if last_pair:
-                    store_bank(g, 0)
-                elif not even:
-                    store_pair(g)
+            if new_q == 0:
+                empty_q_pair(new_q, nc.scalar.copy)
+            if g >= 0 and not vector_helps:
+                empty_scores(g, 0, on_vector=False)
 
             if even:
-                if g >= 0 and exists(new_q):
+                if exists(new_q) and new_q > 0:
                     empty_q_pair(new_q, nc.vector.tensor_copy)
                 if exists(new_k) and vector_empties_k(new_k, g):
                     empty_k(new_k, nc.vector.tensor_copy)
             else:
-                new_w = (g + W_AHEAD) // 2
+                if vector_helps:
+                    empty_scores(g, 0, on_vector=True)
+                if exists(2 * (new_w - 1)):
+                    quantise_weights(new_w - 1)
+                if exists(2 * new_w):
+                    regroup_weights(new_w)
                 if exists(new_k - 2) and (new_k - 2) % PACK == PACK - 1:
                     quantise_k((new_k - 2) // PACK)
                 if exists(new_q - 1):
                     quantise_q_pair(new_q - 1)
-                if exists(2 * (new_w - 1)):
-                    quantise_weights(new_w - 1)
-                if exists(2 * new_w):
-                    regroup_weights(new_w, nc.vector.tensor_copy if g < 0 else gpsimd_copy)
+
+            if g >= 0:
+                store_unit(g)

@@ -11,6 +11,7 @@ U8 = mybir.dt.uint8
 FP8X4 = mybir.dt.float8_e4m3fn_x4
 
 COPY = mybir.ActivationFunctionType.Copy
+ALU = mybir.AluOpType
 
 P = 128
 PACK = 4
@@ -20,10 +21,20 @@ CHUNKS = T // P
 UNITS = H * CHUNKS
 GROUP = P * PACK
 
-Q_AHEAD = 4
-K_AHEAD = CHUNKS + 4
-W_AHEAD = K_AHEAD + 3
-VECTOR_TURN = 4
+FIRST = 12
+SC = 0
+QP = 1
+LAG = 0
+W_EXTRA = (0, 2)
+WB = 2
+GPSIMD_FROM = 4
+GSPLIT = 2
+X_ORDER = (0, 2, 4, 6, 1, 3, 5, 7)
+U0 = 2
+EARLY = 1
+QQ = 0
+S1 = 1
+EF = 0
 
 SCALE = 1.0 / math.sqrt(T)
 
@@ -39,6 +50,7 @@ def tile_multiheadattention_pa_kernel(tc, x, wq, wk, out):
     with ExitStack() as ctx:
         keep = ctx.enter_context(tc.tile_pool(name="keep", bufs=1))
         stage = ctx.enter_context(tc.tile_pool(name="stage", bufs=3))
+        single = ctx.enter_context(tc.tile_pool(name="single", bufs=WB))
         results = ctx.enter_context(tc.tile_pool(name="results", bufs=8))
         psum = ctx.enter_context(tc.psum_pool(name="psum", bufs=8))
         ctx.enter_context(tc.manual_schedule())
@@ -56,9 +68,10 @@ def tile_multiheadattention_pa_kernel(tc, x, wq, wk, out):
         x_raw = []
         for a in range(CHUNKS // 2):
             piece = keep.tile([P, 2 * E], BF16, name="x_raw%d" % a)
+            first_chunk = X_ORDER[2 * a]
             nc.sync.dma_start(
                 out=piece[:].rearrange("p (r e) -> p r e", r=2),
-                in_=x_rows[:, 2 * a : 2 * a + 2, :],
+                in_=x_rows[:, first_chunk : first_chunk + 3 : 2, :],
             )
             x_raw.append(piece)
         w_raw.append(load_weights(wq, 0, "wq"))
@@ -100,24 +113,25 @@ def tile_multiheadattention_pa_kernel(tc, x, wq, wk, out):
         q_mx = [mx_operand("q%d" % h, T) for h in range(H)]
         k_mx = [mx_operand("k%d" % h, T) for h in range(H)]
 
-        def prepare_x():
-            x_grouped = []
-            for a in range(CHUNKS // 2):
-                words = x_raw[a][:].bitcast(F32)
-                bank = psum.tile([P, 2, 2, P], F32, tag="bank", name="x_bank%d" % a)
-                for r in range(2):
-                    for u in range(2):
-                        nc.tensor.transpose(
-                            bank[:, r, u, :], words[:, columns(2 * r + u, P)], identity[:]
-                        )
-                grouped = keep.tile([P, 2 * GROUP], BF16, name="x_grouped%d" % a, align_bytes=64)
-                nc.scalar.copy(
-                    out=grouped[:].bitcast(F32).rearrange("p (r t u) -> p r t u", r=2, u=2),
-                    in_=bank[:].rearrange("p r u t -> p r t u"),
-                )
-                x_grouped.append(grouped)
-            for a in range(CHUNKS // 2):
-                quantise(x_grouped[a], x_mx, columns(a, 2 * P))
+        x_grouped = {}
+
+        def x_columns(r):
+            return columns(X_ORDER.index(r), P)
+
+        def transpose_x(a):
+            words = x_raw[a][:].bitcast(F32)
+            bank = psum.tile([P, 2, 2, P], F32, tag="bank", name="x_bank%d" % a)
+            for r in range(2):
+                for u in range(2):
+                    nc.tensor.transpose(
+                        bank[:, r, u, :], words[:, columns(2 * r + u, P)], identity[:]
+                    )
+            grouped = keep.tile([P, 2 * GROUP], BF16, name="x_grouped%d" % a, align_bytes=64)
+            nc.scalar.copy(
+                out=grouped[:].bitcast(F32).rearrange("p (r t u) -> p r t u", r=2, u=2),
+                in_=bank[:].rearrange("p r u t -> p r t u"),
+            )
+            x_grouped[a] = grouped
 
         w_grouped = {}
         q_bank, q_grouped = {}, {}
@@ -127,19 +141,37 @@ def tile_multiheadattention_pa_kernel(tc, x, wq, wk, out):
         def regroup_weights(n):
             matrix, half = divmod(n, 2)
             raw = w_raw[matrix]
-            grouped = stage.tile(
+            late = n >= GPSIMD_FROM
+            grouped = single.tile(
                 [P, 2 * GROUP], BF16, tag="w_grouped", name="w_grouped%d" % n, align_bytes=64
             )
             if matrix % 2 == 0:
-                nc.vector.tensor_copy(
-                    out=grouped[:].rearrange("p (n i t) -> p n t i", i=4, t=PACK),
-                    in_=raw[:, :, columns(half, 2 * P)].rearrange("p t (n i) -> p n t i", i=4),
-                )
+                src = raw[:, :, columns(half, 2 * P)]
+                if late:
+                    src = src.rearrange("p t n -> p n t")
+                    dst = grouped[:].rearrange("p (n t) -> p n t", t=PACK)
+                else:
+                    src = src.rearrange("p t (n i) -> p n t i", i=4)
+                    dst = grouped[:].rearrange("p (n i t) -> p n t i", i=4, t=PACK)
             else:
-                nc.vector.tensor_copy(
-                    out=grouped[:].rearrange("p (c m t) -> p c m t", c=2, t=PACK),
-                    in_=raw[:].rearrange("p t (m c) -> p c m t", c=PACK)[:, 2 * half : 2 * half + 2],
-                )
+                dst = grouped[:].rearrange("p (c m t) -> p c m t", c=2, t=PACK)
+                src = raw[:].rearrange("p t (m c) -> p c m t", c=PACK)[:, 2 * half : 2 * half + 2]
+            if late:
+                for s in range(GSPLIT):
+                    if matrix % 2 == 0:
+                        part = columns(s, 2 * P // GSPLIT)
+                        d2, s2 = dst[:, part], src[:, part]
+                    elif GSPLIT == 4:
+                        part = columns(s % 2, P // 2)
+                        d2, s2 = dst[:, s // 2, part], src[:, s // 2, part]
+                    else:
+                        part = columns(s, 2 // GSPLIT)
+                        d2, s2 = dst[:, part], src[:, part]
+                    nc.gpsimd.tensor_scalar(
+                        out=d2, in0=s2, scalar1=1.0, scalar2=0.0, op0=ALU.mult, op1=ALU.add
+                    )
+            else:
+                nc.vector.tensor_copy(out=dst, in_=src)
             w_grouped[n] = grouped
 
         def quantise_weights(n):
@@ -152,31 +184,30 @@ def tile_multiheadattention_pa_kernel(tc, x, wq, wk, out):
                 in_=bank[:].rearrange("p c n -> p n c"),
             )
 
-        def project_q(g):
-            h, r = divmod(g, CHUNKS)
-            bank = psum.tile([P, PACK, P], F32, tag="bank", name="q_bank%d" % g)
+        def project_q(m):
+            h, r = divmod(m, CHUNKS)
+            bank = psum.tile([P, PACK, P], F32, tag="bank", name="q_bank%d" % m)
             for c in range(PACK):
-                mx_product(bank[:, c, :], w_mx[2 * h + 1], columns(c, P), x_mx, columns(r, P))
-            q_bank[g] = bank
+                mx_product(bank[:, c, :], w_mx[2 * h + 1], columns(c, P), x_mx, x_columns(r))
+            q_bank[m] = bank
 
-        def empty_q_pair(g, copy_out):
-            grouped = stage.tile(
-                [P, 2 * GROUP], BF16, tag="q_grouped", name="q_grouped%d" % g, align_bytes=64
-            )
-            empty_projection(copy_out, q_bank[g + 1], grouped, 1)
-            empty_projection(copy_out, q_bank[g], grouped, 0)
-            q_grouped[g] = grouped
+        def empty_q(m, copy_out):
+            if m % 2 == 0:
+                q_grouped[m // 2] = stage.tile(
+                    [P, 2 * GROUP], BF16, tag="q_grouped", name="q_grouped%d" % m, align_bytes=64
+                )
+            empty_projection(copy_out, q_bank[m], q_grouped[m // 2], m % 2)
 
-        def quantise_q_pair(g):
-            h, r = divmod(g, CHUNKS)
-            quantise(q_grouped[g], q_mx[h], columns(r // 2, 2 * P))
+        def quantise_q(pair):
+            h, j = divmod(pair, CHUNKS // 2)
+            quantise(q_grouped[pair], q_mx[h], columns(j, 2 * P))
 
         def project_k(n):
             h, j_chunk = divmod(n, CHUNKS)
             jh, b = divmod(j_chunk, PACK)
             bank = psum.tile([P, PACK, P], F32, tag="bank", name="k_bank%d" % n)
             for c in range(PACK):
-                mx_product(bank[:, c, :], x_mx, columns(2 * c + jh, P), w_mx[2 * h], columns(b, P))
+                mx_product(bank[:, c, :], x_mx, x_columns(2 * c + jh), w_mx[2 * h], columns(b, P))
             k_bank[n] = bank
 
         def empty_k(n, copy_out):
@@ -189,75 +220,150 @@ def tile_multiheadattention_pa_kernel(tc, x, wq, wk, out):
         def quantise_k(half):
             quantise(k_grouped[half], k_mx[half // 2], columns(half % 2, BANK))
 
-        def multiply_scores(g):
-            h, r = divmod(g, CHUNKS)
-            for jh in range(T // BANK):
-                bank = psum.tile([P, BANK], F32, tag="bank", name="s_bank%d_%d" % (g, jh))
-                mx_product(bank[:], q_mx[h], columns(r, P), k_mx[h], columns(jh, BANK))
-                s_bank[(g, jh)] = bank
+        def place(u):
+            h, rest = divmod(u, CHUNKS)
+            jh, j = divmod(rest, CHUNKS // 2)
+            return h, jh, j
 
-        def empty_scores(g, jh, on_vector):
-            half_rows = result_of[g][:, columns(jh, BANK)]
+        def multiply_scores(u):
+            h, jh, j = place(u)
+            for i in range(2):
+                bank = psum.tile([P, BANK], F32, tag="bank", name="s_bank%d_%d" % (u, i))
+                mx_product(bank[:], q_mx[h], columns(2 * j + i, P), k_mx[h], columns(jh, BANK))
+                s_bank[(u, i)] = bank
+
+        def empty_scores(u, i, on_vector):
+            rows = result_of[u][:, i, :]
             if on_vector:
-                nc.vector.tensor_scalar_mul(out=half_rows, in0=s_bank[(g, jh)][:], scalar1=SCALE)
+                nc.vector.tensor_scalar_mul(out=rows, in0=s_bank[(u, i)][:], scalar1=SCALE)
             else:
-                nc.scalar.activation(out=half_rows, in_=s_bank[(g, jh)][:], func=COPY, scale=SCALE)
+                nc.scalar.activation(out=rows, in_=s_bank[(u, i)][:], func=COPY, scale=SCALE)
 
         out_rows = [out[h, 0].rearrange("(p r) j -> p r j", r=CHUNKS) for h in range(H)]
 
-        def store_unit(g):
-            h, r = divmod(g, CHUNKS)
-            nc.sync.dma_start(out=out_rows[h][:, r, :], in_=result_of[g][:])
+        def store_unit(u):
+            h, jh, j = place(u)
+            nc.sync.dma_start(
+                out=out_rows[h][:, 2 * j : 2 * j + 2, columns(jh, BANK)], in_=result_of[u][:]
+            )
 
         def exists(i):
             return 0 <= i < UNITS
 
-        def vector_empties_k(n, g):
-            return g >= 0 and n % VECTOR_TURN == 0
-
-        for g in range(-W_AHEAD, UNITS):
-            even = g % 2 == 0
-            new_k = g + K_AHEAD
-            new_q = g + Q_AHEAD
-            new_w = (g + W_AHEAD) // 2
-            vector_helps = g >= 0 and not even and not exists(2 * new_w)
-            if new_k == 0:
-                prepare_x()
-
-            if g >= 0:
-                multiply_scores(g)
-            if exists(new_k):
-                project_k(new_k)
-            if even and exists(new_q):
-                project_q(new_q)
-                project_q(new_q + 1)
-
-            if g >= 0:
-                result_of[g] = results.tile([P, T], F32, tag="result", name="result%d" % g)
-                empty_scores(g, 1, on_vector=False)
-            if exists(new_k - 1) and not vector_empties_k(new_k - 1, g - 1):
-                empty_k(new_k - 1, nc.scalar.copy)
-            if new_q == 0:
-                empty_q_pair(new_q, nc.scalar.copy)
-            if g >= 0 and not vector_helps:
-                empty_scores(g, 0, on_vector=False)
-
-            if even:
-                if exists(new_q) and new_q > 0:
-                    empty_q_pair(new_q, nc.vector.tensor_copy)
-                if exists(new_k) and vector_empties_k(new_k, g):
-                    empty_k(new_k, nc.vector.tensor_copy)
+        def need(kind, n):
+            if kind == 0:
+                return 0 if n < CHUNKS else 4 * (n // PACK)
+            return CHUNKS * (n // CHUNKS) + (n % CHUNKS) // 2
+        order = sorted([(need(k, n), k, n) for k in (0, 1) for n in range(UNITS)])
+        def project(i):
+            kind, n = order[i][1:]
+            if kind == 0:
+                project_k(n)
             else:
-                if vector_helps:
-                    empty_scores(g, 0, on_vector=True)
-                if exists(2 * (new_w - 1)):
-                    quantise_weights(new_w - 1)
-                if exists(2 * new_w):
-                    regroup_weights(new_w)
-                if exists(new_k - 2) and (new_k - 2) % PACK == PACK - 1:
-                    quantise_k((new_k - 2) // PACK)
-                if exists(new_q - 1):
-                    quantise_q_pair(new_q - 1)
+                project_q(n)
 
-            if g >= 0:
-                store_unit(g)
+        quants = []
+        copied = {}
+
+        def empty(i, copy_out):
+            kind, n = order[i][1:]
+            if kind == 0:
+                empty_k(n, copy_out)
+                group = (0, n // PACK)
+            else:
+                empty_q(n, copy_out)
+                group = (1, n // 2)
+            copied[group] = copied.get(group, 0) + 1
+            if copied[group] == (PACK if kind == 0 else 2):
+                quants.append(group)
+
+        def quantise_group(group):
+            if group[0] == 0:
+                quantise_k(group[1])
+            else:
+                quantise_q(group[1])
+
+        on_scalar, on_vector = nc.scalar.copy, nc.vector.tensor_copy
+        regroup_weights(0)
+        regroup_weights(1)
+        for a in range(4):
+            transpose_x(a)
+        quantise_weights(0)
+        quantise_weights(1)
+        for a in range(2):
+            quantise(x_grouped[a], x_mx, columns(a, 2 * P))
+        for i in range(4):
+            project(i)
+        for a in range(2, 4):
+            quantise(x_grouped[a], x_mx, columns(a, 2 * P))
+        regroup_weights(2)
+        regroup_weights(3)
+        for i in range(4, 8):
+            project(i)
+        for i in range(6):
+            empty(i, on_scalar)
+        quantise_weights(3)
+        quantise_weights(2)
+        quantise_group(quants.pop(0))
+        regroup_weights(4)
+        for i in range(8, FIRST):
+            project(i)
+        empty(8, on_vector)
+        if S1:
+            empty(9, on_scalar)
+            empty(6, on_scalar)
+        else:
+            empty(6, on_scalar)
+            empty(9, on_scalar)
+        empty(7, on_vector)
+        late_k = [g for g in quants if g[0] == 0][0]
+        quants.remove(late_k)
+        quantise_group(quants.pop(0))
+        quants.append(late_k)
+        regroup_weights(5)
+        for i in range(10, FIRST - LAG):
+            empty(i, on_vector if i % 2 == 0 else on_scalar)
+            if QQ and i % 2 == 1:
+                quantise_group(quants.pop(0))
+        if not QQ and EF:
+            for g in quants[:]:
+                quantise_group(g)
+            quants.clear()
+        quantise_weights(4)
+        next_w = 5
+        for n in range(6, 5 + WB):
+            regroup_weights(n)
+        for u in range(UNITS):
+            first = FIRST + 2 * u
+            total = len(order)
+            busy = first < total
+            multiply_scores(u)
+            for i in range(first, first + 2):
+                if i < total:
+                    project(i)
+            result_of[u] = results.tile([P, 2, BANK], F32, tag="result", name="result%d" % u)
+            empty_scores(u, 0, on_vector=False)
+            empty_scores(u, 1, on_vector=not busy)
+            if u % 2 == 0 or u < U0:
+                ready = quants[:]
+            if u < U0 and EARLY:
+                for g in ready:
+                    quantise_group(g)
+                    quants.remove(g)
+                ready = []
+            for i in range(first - LAG, first - LAG + 2):
+                if i < total:
+                    empty(i, on_scalar if i % 4 == SC else on_vector)
+                    if u % 2 == 1 and i == first - LAG + QP:
+                        ready = quants[:]
+            if u % 2 == 1 or not busy or u < U0:
+                for g in (ready if busy else quants[:]):
+                    quantise_group(g)
+                    quants.remove(g)
+            if u % 2 == 1 or u in W_EXTRA:
+                if next_w < 4 * H:
+                    quantise_weights(next_w)
+                    next_w += 1
+                    if next_w + WB - 1 < 4 * H:
+                        regroup_weights(next_w + WB - 1)
+            store_unit(u)

@@ -22,13 +22,13 @@ UNITS = H * CHUNKS
 GROUP = P * PACK
 
 FIRST = 12
-SC = 0
+SC = (0, 4)
 QP = 1
 LAG = 0
 W_EXTRA = (0, 2)
 WB = 2
 GPSIMD_FROM = 4
-GSPLIT = 2
+GSPLIT = 1
 X_ORDER = (0, 2, 4, 6, 1, 3, 5, 7)
 U0 = 2
 EARLY = 1
@@ -353,7 +353,7 @@ def tile_multiheadattention_pa_kernel(tc, x, wq, wk, out):
                 ready = []
             for i in range(first - LAG, first - LAG + 2):
                 if i < total:
-                    empty(i, on_scalar if i % 4 == SC else on_vector)
+                    empty(i, on_scalar if i % 8 in SC else on_vector)
                     if u % 2 == 1 and i == first - LAG + QP:
                         ready = quants[:]
             if u % 2 == 1 or not busy or u < U0:

@@ -27,14 +27,17 @@ QP = 1
 LAG = 0
 W_EXTRA = (0, 2)
 WB = 2
-GPSIMD_FROM = 4
+GPSIMD_FROM = 6
 GSPLIT = 1
 X_ORDER = (0, 2, 4, 6, 1, 3, 5, 7)
 U0 = 2
 EARLY = 1
 QQ = 0
 S1 = 1
-EF = 0
+EF = 1
+NEWEST = 1
+NEWV = 1
+RB = 24
 
 SCALE = 1.0 / math.sqrt(T)
 
@@ -51,7 +54,7 @@ def tile_multiheadattention_pa_kernel(tc, x, wq, wk, out):
         keep = ctx.enter_context(tc.tile_pool(name="keep", bufs=1))
         stage = ctx.enter_context(tc.tile_pool(name="stage", bufs=3))
         single = ctx.enter_context(tc.tile_pool(name="single", bufs=WB))
-        results = ctx.enter_context(tc.tile_pool(name="results", bufs=8))
+        results = ctx.enter_context(tc.tile_pool(name="results", bufs=RB))
         psum = ctx.enter_context(tc.psum_pool(name="psum", bufs=8))
         ctx.enter_context(tc.manual_schedule())
 
@@ -192,7 +195,7 @@ def tile_multiheadattention_pa_kernel(tc, x, wq, wk, out):
             q_bank[m] = bank
 
         def empty_q(m, copy_out):
-            if m % 2 == 0:
+            if m // 2 not in q_grouped:
                 q_grouped[m // 2] = stage.tile(
                     [P, 2 * GROUP], BF16, tag="q_grouped", name="q_grouped%d" % m, align_bytes=64
                 )
@@ -211,7 +214,7 @@ def tile_multiheadattention_pa_kernel(tc, x, wq, wk, out):
             k_bank[n] = bank
 
         def empty_k(n, copy_out):
-            if n % PACK == 0:
+            if n // PACK not in k_grouped:
                 k_grouped[n // PACK] = stage.tile(
                     [P, PACK * GROUP], BF16, tag="k_grouped", name="k_grouped%d" % n, align_bytes=64
                 )
@@ -342,8 +345,12 @@ def tile_multiheadattention_pa_kernel(tc, x, wq, wk, out):
                 if i < total:
                     project(i)
             result_of[u] = results.tile([P, 2, BANK], F32, tag="result", name="result%d" % u)
-            empty_scores(u, 0, on_vector=False)
-            empty_scores(u, 1, on_vector=not busy)
+            if NEWEST:
+                empty_scores(u, 1, on_vector=False)
+                empty_scores(u, 0, on_vector=not busy)
+            else:
+                empty_scores(u, 0, on_vector=False)
+                empty_scores(u, 1, on_vector=not busy)
             if u % 2 == 0 or u < U0:
                 ready = quants[:]
             if u < U0 and EARLY:
@@ -351,10 +358,10 @@ def tile_multiheadattention_pa_kernel(tc, x, wq, wk, out):
                     quantise_group(g)
                     quants.remove(g)
                 ready = []
-            for i in range(first - LAG, first - LAG + 2):
+            for i in (range(first - LAG + 1, first - LAG - 1, -1) if NEWV else range(first - LAG, first - LAG + 2)):
                 if i < total:
                     empty(i, on_scalar if i % 8 in SC else on_vector)
-                    if u % 2 == 1 and i == first - LAG + QP:
+                    if u % 2 == 1 and QP and i == (first - LAG if NEWV else first - LAG + 1):
                         ready = quants[:]
             if u % 2 == 1 or not busy or u < U0:
                 for g in (ready if busy else quants[:]):

@@ -27,17 +27,19 @@ QP = 1
 LAG = 0
 W_EXTRA = (0, 2)
 WB = 2
-GPSIMD_FROM = 6
+GPSIMD_FROM = 4
 GSPLIT = 1
 X_ORDER = (0, 2, 4, 6, 1, 3, 5, 7)
 U0 = 2
 EARLY = 1
-QQ = 0
-S1 = 1
-EF = 1
 NEWEST = 1
-NEWV = 1
+NEWV = 0
 RB = 24
+GS = range(10, 16)
+WPOS = 1
+R4 = 0
+K7 = 0
+AC = (12, 13, 16)
 
 SCALE = 1.0 / math.sqrt(T)
 
@@ -144,7 +146,7 @@ def tile_multiheadattention_pa_kernel(tc, x, wq, wk, out):
         def regroup_weights(n):
             matrix, half = divmod(n, 2)
             raw = w_raw[matrix]
-            late = n >= GPSIMD_FROM
+            late = n in GS
             grouped = single.tile(
                 [P, 2 * GROUP], BF16, tag="w_grouped", name="w_grouped%d" % n, align_bytes=64
             )
@@ -308,30 +310,24 @@ def tile_multiheadattention_pa_kernel(tc, x, wq, wk, out):
         quantise_weights(3)
         quantise_weights(2)
         quantise_group(quants.pop(0))
-        regroup_weights(4)
         for i in range(8, FIRST):
             project(i)
         empty(8, on_vector)
-        if S1:
-            empty(9, on_scalar)
-            empty(6, on_scalar)
-        else:
-            empty(6, on_scalar)
-            empty(9, on_scalar)
-        empty(7, on_vector)
-        late_k = [g for g in quants if g[0] == 0][0]
-        quants.remove(late_k)
+        empty(9, on_scalar)
+        empty(11, on_scalar)
+        empty(10, on_vector)
+        empty(6, on_scalar)
+        if R4 == 0:
+            regroup_weights(4)
         quantise_group(quants.pop(0))
-        quants.append(late_k)
+        quantise_group(quants.pop(0))
+        if R4 == 1:
+            regroup_weights(4)
+        if K7 == 0:
+            empty(7, on_scalar)
+        elif K7 == 1:
+            empty(7, on_vector)
         regroup_weights(5)
-        for i in range(10, FIRST - LAG):
-            empty(i, on_vector if i % 2 == 0 else on_scalar)
-            if QQ and i % 2 == 1:
-                quantise_group(quants.pop(0))
-        if not QQ and EF:
-            for g in quants[:]:
-                quantise_group(g)
-            quants.clear()
         quantise_weights(4)
         next_w = 5
         for n in range(6, 5 + WB):
@@ -360,16 +356,24 @@ def tile_multiheadattention_pa_kernel(tc, x, wq, wk, out):
                 ready = []
             for i in (range(first - LAG + 1, first - LAG - 1, -1) if NEWV else range(first - LAG, first - LAG + 2)):
                 if i < total:
-                    empty(i, on_scalar if i % 8 in SC else on_vector)
+                    empty(i, on_scalar if (i in AC if i < 20 else i % 8 in SC) else on_vector)
                     if u % 2 == 1 and QP and i == (first - LAG if NEWV else first - LAG + 1):
                         ready = quants[:]
             if u % 2 == 1 or not busy or u < U0:
-                for g in (ready if busy else quants[:]):
+                due = ready if busy else quants[:]
+                w_now = (u % 2 == 1 or u in W_EXTRA) and next_w < 4 * H
+                for x, g in enumerate(due):
+                    if WPOS and w_now and x == len(due) - 1:
+                        quantise_weights(next_w)
                     quantise_group(g)
                     quants.remove(g)
+                w_done = WPOS and w_now and len(due) > 0
+            else:
+                w_done = False
             if u % 2 == 1 or u in W_EXTRA:
                 if next_w < 4 * H:
-                    quantise_weights(next_w)
+                    if not w_done:
+                        quantise_weights(next_w)
                     next_w += 1
                     if next_w + WB - 1 < 4 * H:
                         regroup_weights(next_w + WB - 1)

@@ -22,24 +22,27 @@ UNITS = H * CHUNKS
 GROUP = P * PACK
 
 FIRST = 12
-SC = (0, 4)
-QP = 1
+SC = (4,)
 LAG = 0
-W_EXTRA = (0, 2)
-WB = 2
+ORD = 1
+SLOW = 25
+VH = 26
+W_EXTRA = (0,2)
+WL = 1
+WV = 3
 GPSIMD_FROM = 4
 GSPLIT = 1
 X_ORDER = (0, 2, 4, 6, 1, 3, 5, 7)
 U0 = 2
 EARLY = 1
-NEWEST = 1
+NEWEST = 0
 NEWV = 0
 RB = 24
-GS = range(10, 16)
+GS = range(8,16)
 WPOS = 1
-R4 = 0
+R4 = 1
 K7 = 0
-AC = (12, 13, 16)
+AC = (12,13,14,16)
 
 SCALE = 1.0 / math.sqrt(T)
 
@@ -55,7 +58,7 @@ def tile_multiheadattention_pa_kernel(tc, x, wq, wk, out):
     with ExitStack() as ctx:
         keep = ctx.enter_context(tc.tile_pool(name="keep", bufs=1))
         stage = ctx.enter_context(tc.tile_pool(name="stage", bufs=3))
-        single = ctx.enter_context(tc.tile_pool(name="single", bufs=WB))
+        single = ctx.enter_context(tc.tile_pool(name="single", bufs=1))
         results = ctx.enter_context(tc.tile_pool(name="results", bufs=RB))
         psum = ctx.enter_context(tc.psum_pool(name="psum", bufs=8))
         ctx.enter_context(tc.manual_schedule())
@@ -147,8 +150,8 @@ def tile_multiheadattention_pa_kernel(tc, x, wq, wk, out):
             matrix, half = divmod(n, 2)
             raw = w_raw[matrix]
             late = n in GS
-            grouped = single.tile(
-                [P, 2 * GROUP], BF16, tag="w_grouped", name="w_grouped%d" % n, align_bytes=64
+            grouped = stage.tile(
+                [P, 2 * GROUP], BF16, tag="w_late" if late else "w_early", name="w_grouped%d" % n, align_bytes=64, bufs=WL if late else WV
             )
             if matrix % 2 == 0:
                 src = raw[:, :, columns(half, 2 * P)]
@@ -227,7 +230,12 @@ def tile_multiheadattention_pa_kernel(tc, x, wq, wk, out):
 
         def place(u):
             h, rest = divmod(u, CHUNKS)
-            jh, j = divmod(rest, CHUNKS // 2)
+            if ORD == 0:
+                jh, j = divmod(rest, CHUNKS // 2)
+            else:
+                a, rest = divmod(rest, 4)
+                jh, b = divmod(rest, 2)
+                j = 2 * a + b
             return h, jh, j
 
         def multiply_scores(u):
@@ -257,8 +265,9 @@ def tile_multiheadattention_pa_kernel(tc, x, wq, wk, out):
 
         def need(kind, n):
             if kind == 0:
-                return 0 if n < CHUNKS else 4 * (n // PACK)
-            return CHUNKS * (n // CHUNKS) + (n % CHUNKS) // 2
+                return 0 if n < CHUNKS else (4 * (n // PACK) if ORD == 0 else CHUNKS * (n // CHUNKS) + 2 * (n % CHUNKS // PACK))
+            j = n % CHUNKS // 2
+            return CHUNKS * (n // CHUNKS) + (j if ORD == 0 else 4 * (j // 2) + j % 2)
         order = sorted([(need(k, n), k, n) for k in (0, 1) for n in range(UNITS)])
         def project(i):
             kind, n = order[i][1:]
@@ -330,23 +339,27 @@ def tile_multiheadattention_pa_kernel(tc, x, wq, wk, out):
         regroup_weights(5)
         quantise_weights(4)
         next_w = 5
-        for n in range(6, 5 + WB):
-            regroup_weights(n)
+        regrouped = 6
+        while regrouped < next_w + (WL if regrouped in GS else WV):
+            regroup_weights(regrouped)
+            regrouped += 1
+        done = FIRST
         for u in range(UNITS):
-            first = FIRST + 2 * u
             total = len(order)
+            first = done
+            done = min(total, done + (1 if u >= SLOW else 2))
             busy = first < total
+            vhelp = not busy or u >= VH
             multiply_scores(u)
-            for i in range(first, first + 2):
-                if i < total:
-                    project(i)
+            for i in range(first, done):
+                project(i)
             result_of[u] = results.tile([P, 2, BANK], F32, tag="result", name="result%d" % u)
             if NEWEST:
                 empty_scores(u, 1, on_vector=False)
-                empty_scores(u, 0, on_vector=not busy)
+                empty_scores(u, 0, on_vector=vhelp)
             else:
                 empty_scores(u, 0, on_vector=False)
-                empty_scores(u, 1, on_vector=not busy)
+                empty_scores(u, 1, on_vector=vhelp)
             if u % 2 == 0 or u < U0:
                 ready = quants[:]
             if u < U0 and EARLY:
@@ -354,10 +367,10 @@ def tile_multiheadattention_pa_kernel(tc, x, wq, wk, out):
                     quantise_group(g)
                     quants.remove(g)
                 ready = []
-            for i in (range(first - LAG + 1, first - LAG - 1, -1) if NEWV else range(first - LAG, first - LAG + 2)):
+            for i in (range(done - 1, first - 1, -1) if NEWV else range(first, done)):
                 if i < total:
                     empty(i, on_scalar if (i in AC if i < 20 else i % 8 in SC) else on_vector)
-                    if u % 2 == 1 and QP and i == (first - LAG if NEWV else first - LAG + 1):
+                    if u % 2 == 1 and i == (first if NEWV else done - 1):
                         ready = quants[:]
             if u % 2 == 1 or not busy or u < U0:
                 due = ready if busy else quants[:]
@@ -375,6 +388,7 @@ def tile_multiheadattention_pa_kernel(tc, x, wq, wk, out):
                     if not w_done:
                         quantise_weights(next_w)
                     next_w += 1
-                    if next_w + WB - 1 < 4 * H:
-                        regroup_weights(next_w + WB - 1)
+                    while regrouped < 4 * H and regrouped < next_w + (WL if regrouped in GS else WV) :
+                        regroup_weights(regrouped)
+                        regrouped += 1
             store_unit(u)

@@ -22,10 +22,10 @@ UNITS = H * CHUNKS
 GROUP = P * PACK
 
 FIRST = 12
-SC = (4,)
+SC = (2,)
 LAG = 0
 ORD = 1
-SLOW = 25
+SLOW = 24
 VH = 26
 W_EXTRA = (0,2)
 WL = 1
@@ -34,15 +34,28 @@ GPSIMD_FROM = 4
 GSPLIT = 1
 X_ORDER = (0, 2, 4, 6, 1, 3, 5, 7)
 U0 = 2
-EARLY = 1
+EARLY = 0
+EARLY1 = 0
+SINGLE = 16
+SINGLE_END = 1
 NEWEST = 0
 NEWV = 0
-RB = 24
+RB = 11
 GS = range(8,16)
 WPOS = 1
-R4 = 1
+R4 = 0
 K7 = 0
 AC = (12,13,14,16)
+SAME = 0
+SPLIT = 0
+QF = 0
+A5 = 0
+PEO = 0
+ACO = 3
+MERGED = (2,3)
+MH = 1
+MQ = 1
+SCM = 5
 
 SCALE = 1.0 / math.sqrt(T)
 
@@ -146,12 +159,30 @@ def tile_multiheadattention_pa_kernel(tc, x, wq, wk, out):
         k_bank, k_grouped = {}, {}
         s_bank, result_of = {}, {}
 
+        def regroup_whole(matrix):
+            raw = w_raw[matrix]
+            grouped = stage.tile(
+                [P, 4 * GROUP], BF16, tag="w_whole", name="w_whole%d" % matrix, align_bytes=64, bufs=2
+            )
+            if matrix % 2 == 0:
+                src = raw[:].rearrange("p t (n i) -> p n t i", i=4)
+                dst = grouped[:].rearrange("p (n i t) -> p n t i", i=4, t=PACK)
+            else:
+                dst = grouped[:].rearrange("p (c m t) -> p c m t", c=4, t=PACK)
+                src = raw[:].rearrange("p t (m c) -> p c m t", c=PACK)
+            nc.vector.tensor_copy(out=dst, in_=src)
+            w_grouped[2 * matrix] = grouped
+
         def regroup_weights(n):
             matrix, half = divmod(n, 2)
+            if matrix in MERGED:
+                if half == MH:
+                    regroup_whole(matrix)
+                return
             raw = w_raw[matrix]
             late = n in GS
             grouped = stage.tile(
-                [P, 2 * GROUP], BF16, tag="w_late" if late else "w_early", name="w_grouped%d" % n, align_bytes=64, bufs=WL if late else WV
+                [P, 2 * GROUP], BF16, tag="w_late" if late and not SAME else "w_early", name="w_grouped%d" % n, align_bytes=64, bufs=WL if late and not SAME else WV
             )
             if matrix % 2 == 0:
                 src = raw[:, :, columns(half, 2 * P)]
@@ -184,6 +215,10 @@ def tile_multiheadattention_pa_kernel(tc, x, wq, wk, out):
 
         def quantise_weights(n):
             matrix, half = divmod(n, 2)
+            if matrix in MERGED:
+                if half == MQ:
+                    quantise(w_grouped[2 * matrix], w_mx[matrix], slice(0, E))
+                return
             quantise(w_grouped[n], w_mx[matrix], columns(half, 2 * P))
 
         def empty_projection(copy_out, bank, grouped, place):
@@ -230,23 +265,23 @@ def tile_multiheadattention_pa_kernel(tc, x, wq, wk, out):
 
         def place(u):
             h, rest = divmod(u, CHUNKS)
-            if ORD == 0:
-                jh, j = divmod(rest, CHUNKS // 2)
-            else:
-                a, rest = divmod(rest, 4)
-                jh, b = divmod(rest, 2)
-                j = 2 * a + b
-            return h, jh, j
+            if ORD == 2:
+                return h, [(rest, 0), (rest, 1)]
+            a, rest = divmod(rest, 4)
+            jh, b = divmod(rest, 2)
+            j = 2 * a + b
+            return h, [(2 * j, jh), (2 * j + 1, jh)]
 
-        def multiply_scores(u):
-            h, jh, j = place(u)
-            for i in range(2):
+        def multiply_scores(u, which=(0, 1)):
+            h, banks = place(u)
+            for i in which:
+                r, jh = banks[i]
                 bank = psum.tile([P, BANK], F32, tag="bank", name="s_bank%d_%d" % (u, i))
-                mx_product(bank[:], q_mx[h], columns(2 * j + i, P), k_mx[h], columns(jh, BANK))
+                mx_product(bank[:], q_mx[h], columns(r, P), k_mx[h], columns(jh, BANK))
                 s_bank[(u, i)] = bank
 
         def empty_scores(u, i, on_vector):
-            rows = result_of[u][:, i, :]
+            rows = result_of[u // 2][:, 2 * (u % 2) + i, :]
             if on_vector:
                 nc.vector.tensor_scalar_mul(out=rows, in0=s_bank[(u, i)][:], scalar1=SCALE)
             else:
@@ -255,19 +290,26 @@ def tile_multiheadattention_pa_kernel(tc, x, wq, wk, out):
         out_rows = [out[h, 0].rearrange("(p r) j -> p r j", r=CHUNKS) for h in range(H)]
 
         def store_unit(u):
-            h, jh, j = place(u)
-            nc.sync.dma_start(
-                out=out_rows[h][:, 2 * j : 2 * j + 2, columns(jh, BANK)], in_=result_of[u][:]
-            )
+            h, banks = place(u)
+            r, jh = banks[0]
+            pair = result_of[u // 2]
+            if u // 2 < SINGLE or u // 2 >= UNITS // 2 - SINGLE_END:
+                nc.sync.dma_start(
+                    out=out_rows[h][:, r : r + 2, columns(jh, BANK)], in_=pair[:, columns(u % 2, 2), :]
+                )
+            elif u % 2 == 1:
+                nc.sync.dma_start(out=out_rows[h][:, r - 2 : r + 2, columns(jh, BANK)], in_=pair[:])
 
         def exists(i):
             return 0 <= i < UNITS
 
         def need(kind, n):
-            if kind == 0:
-                return 0 if n < CHUNKS else (4 * (n // PACK) if ORD == 0 else CHUNKS * (n // CHUNKS) + 2 * (n % CHUNKS // PACK))
             j = n % CHUNKS // 2
-            return CHUNKS * (n // CHUNKS) + (j if ORD == 0 else 4 * (j // 2) + j % 2)
+            if ORD == 2:
+                return CHUNKS * (n // CHUNKS) + (0 if kind == 0 else 2 * j)
+            if kind == 0:
+                return 0 if n < CHUNKS else CHUNKS * (n // CHUNKS) + 2 * (n % CHUNKS // PACK)
+            return CHUNKS * (n // CHUNKS) + 4 * (j // 2) + j % 2
         order = sorted([(need(k, n), k, n) for k in (0, 1) for n in range(UNITS)])
         def project(i):
             kind, n = order[i][1:]
@@ -314,7 +356,7 @@ def tile_multiheadattention_pa_kernel(tc, x, wq, wk, out):
         regroup_weights(3)
         for i in range(4, 8):
             project(i)
-        for i in range(6):
+        for i in range(6 - A5):
             empty(i, on_scalar)
         quantise_weights(3)
         quantise_weights(2)
@@ -323,12 +365,19 @@ def tile_multiheadattention_pa_kernel(tc, x, wq, wk, out):
             project(i)
         empty(8, on_vector)
         empty(9, on_scalar)
+        if A5:
+            empty(5, on_scalar)
+        if QF == 2:
+            quantise_group(quants.pop(0))
         empty(11, on_scalar)
         empty(10, on_vector)
+        if QF == 1:
+            quantise_group(quants.pop(0))
         empty(6, on_scalar)
         if R4 == 0:
             regroup_weights(4)
-        quantise_group(quants.pop(0))
+        if not QF:
+            quantise_group(quants.pop(0))
         quantise_group(quants.pop(0))
         if R4 == 1:
             regroup_weights(4)
@@ -336,30 +385,52 @@ def tile_multiheadattention_pa_kernel(tc, x, wq, wk, out):
             empty(7, on_scalar)
         elif K7 == 1:
             empty(7, on_vector)
+        if ORD == 2:
+            quantise_group(quants.pop(0))
         regroup_weights(5)
         quantise_weights(4)
         next_w = 5
         regrouped = 6
-        while regrouped < next_w + (WL if regrouped in GS else WV):
+        while regrouped < next_w + (WL if regrouped in GS and not SAME else WV):
             regroup_weights(regrouped)
             regrouped += 1
         done = FIRST
         for u in range(UNITS):
             total = len(order)
             first = done
-            done = min(total, done + (1 if u >= SLOW else 2))
+            done = min(total, done + (1 if u >= SLOW or u < EARLY1 else 2))
             busy = first < total
             vhelp = not busy or u >= VH
-            multiply_scores(u)
-            for i in range(first, done):
-                project(i)
-            result_of[u] = results.tile([P, 2, BANK], F32, tag="result", name="result%d" % u)
-            if NEWEST:
-                empty_scores(u, 1, on_vector=False)
-                empty_scores(u, 0, on_vector=vhelp)
+            if PEO == 0:
+                multiply_scores(u)
+            if PEO == 2 and done > first:
+                multiply_scores(u, (0,))
+                project(first)
+                multiply_scores(u, (1,))
+                for i in range(first + 1, done):
+                    project(i)
+            elif PEO == 2:
+                multiply_scores(u)
             else:
-                empty_scores(u, 0, on_vector=False)
-                empty_scores(u, 1, on_vector=vhelp)
+                for i in range(first, done):
+                    project(i)
+            if PEO == 1:
+                multiply_scores(u)
+            if u % 2 == 0:
+                result_of[u // 2] = results.tile([P, 4, BANK], F32, tag="result", name="result%d" % u)
+            s_order = ((1, 0) if NEWEST else (0, 1))
+            early_copy = [i for i in range(first, done) if (i in AC if i < 20 else i % SCM in SC)]
+            if ACO == 1:
+                for i in early_copy:
+                    empty(i, on_scalar)
+            empty_scores(u, s_order[0], on_vector=False)
+            if ACO == 2 or ACO == 3 and u >= 2:
+                for i in early_copy:
+                    empty(i, on_scalar)
+            empty_scores(u, s_order[1], on_vector=vhelp)
+            if ACO == 0 or ACO == 3 and u < 2:
+                for i in early_copy:
+                    empty(i, on_scalar)
             if u % 2 == 0 or u < U0:
                 ready = quants[:]
             if u < U0 and EARLY:
@@ -369,7 +440,8 @@ def tile_multiheadattention_pa_kernel(tc, x, wq, wk, out):
                 ready = []
             for i in (range(done - 1, first - 1, -1) if NEWV else range(first, done)):
                 if i < total:
-                    empty(i, on_scalar if (i in AC if i < 20 else i % 8 in SC) else on_vector)
+                    if i not in early_copy:
+                        empty(i, on_vector)
                     if u % 2 == 1 and i == (first if NEWV else done - 1):
                         ready = quants[:]
             if u % 2 == 1 or not busy or u < U0:
@@ -388,7 +460,7 @@ def tile_multiheadattention_pa_kernel(tc, x, wq, wk, out):
                     if not w_done:
                         quantise_weights(next_w)
                     next_w += 1
-                    while regrouped < 4 * H and regrouped < next_w + (WL if regrouped in GS else WV) :
+                    while regrouped < 4 * H and regrouped < next_w + (WL if regrouped in GS and not SAME else WV) :
                         regroup_weights(regrouped)
                         regrouped += 1
             store_unit(u)

@@ -24,7 +24,7 @@ GROUP = P * PACK
 FIRST = 12
 SC = (2,)
 LAG = 0
-ORD = 1
+ORD = 4
 SLOW = 24
 VH = 26
 W_EXTRA = (0,2)
@@ -56,6 +56,7 @@ MERGED = (2,3)
 MH = 1
 MQ = 1
 SCM = 5
+TQ = 24
 
 SCALE = 1.0 / math.sqrt(T)
 
@@ -269,6 +270,8 @@ def tile_multiheadattention_pa_kernel(tc, x, wq, wk, out):
                 return h, [(rest, 0), (rest, 1)]
             a, rest = divmod(rest, 4)
             jh, b = divmod(rest, 2)
+            if a == 1 and ORD == 4:
+                b, jh = jh, b
             j = 2 * a + b
             return h, [(2 * j, jh), (2 * j + 1, jh)]
 
@@ -309,7 +312,7 @@ def tile_multiheadattention_pa_kernel(tc, x, wq, wk, out):
                 return CHUNKS * (n // CHUNKS) + (0 if kind == 0 else 2 * j)
             if kind == 0:
                 return 0 if n < CHUNKS else CHUNKS * (n // CHUNKS) + 2 * (n % CHUNKS // PACK)
-            return CHUNKS * (n // CHUNKS) + 4 * (j // 2) + j % 2
+            return CHUNKS * (n // CHUNKS) + 4 * (j // 2) + j % 2 * (2 if j // 2 and ORD == 4 else 1)
         order = sorted([(need(k, n), k, n) for k in (0, 1) for n in range(UNITS)])
         def project(i):
             kind, n = order[i][1:]
@@ -444,8 +447,8 @@ def tile_multiheadattention_pa_kernel(tc, x, wq, wk, out):
                         empty(i, on_vector)
                     if u % 2 == 1 and i == (first if NEWV else done - 1):
                         ready = quants[:]
-            if u % 2 == 1 or not busy or u < U0:
-                due = ready if busy else quants[:]
+            if u % 2 == 1 or not busy or u < U0 or u >= TQ:
+                due = ready if busy and u < TQ else quants[:]
                 w_now = (u % 2 == 1 or u in W_EXTRA) and next_w < 4 * H
                 for x, g in enumerate(due):
                     if WPOS and w_now and x == len(due) - 1:

@@ -52,11 +52,13 @@ QF = 0
 A5 = 0
 PEO = 0
 ACO = 3
-MERGED = (2,3)
+MERGED = (1,2,3)
 MH = 1
 MQ = 1
 SCM = 5
 TQ = 24
+SCK = 0
+R3 = ()
 
 SCALE = 1.0 / math.sqrt(T)
 
@@ -169,8 +171,8 @@ def tile_multiheadattention_pa_kernel(tc, x, wq, wk, out):
                 src = raw[:].rearrange("p t (n i) -> p n t i", i=4)
                 dst = grouped[:].rearrange("p (n i t) -> p n t i", i=4, t=PACK)
             else:
-                dst = grouped[:].rearrange("p (c m t) -> p c m t", c=4, t=PACK)
-                src = raw[:].rearrange("p t (m c) -> p c m t", c=PACK)
+                dst = grouped[:].rearrange("p (c m t) -> p m t c", c=PACK, t=PACK)
+                src = raw[:].rearrange("p t (m c) -> p m t c", c=PACK)
             nc.vector.tensor_copy(out=dst, in_=src)
             w_grouped[2 * matrix] = grouped
 
@@ -401,7 +403,7 @@ def tile_multiheadattention_pa_kernel(tc, x, wq, wk, out):
         for u in range(UNITS):
             total = len(order)
             first = done
-            done = min(total, done + (1 if u >= SLOW or u < EARLY1 else 2))
+            done = min(total, done + (1 if u >= SLOW or u < EARLY1 else 3 if u in R3 else 2))
             busy = first < total
             vhelp = not busy or u >= VH
             if PEO == 0:
@@ -422,7 +424,7 @@ def tile_multiheadattention_pa_kernel(tc, x, wq, wk, out):
             if u % 2 == 0:
                 result_of[u // 2] = results.tile([P, 4, BANK], F32, tag="result", name="result%d" % u)
             s_order = ((1, 0) if NEWEST else (0, 1))
-            early_copy = [i for i in range(first, done) if (i in AC if i < 20 else i % SCM in SC)]
+            early_copy = [i for i in range(first, done) if (i in AC if i < 20 else (i % SCM in SC if SCK == 0 else order[i][1] == SCK - 1 and order[i][2] % SCM in SC))]
             if ACO == 1:
                 for i in early_copy:
                     empty(i, on_scalar)

from contextlib import ExitStack
import math

import concourse.mybir as mybir
from concourse.masks import make_identity

BF16 = mybir.dt.bfloat16
F32 = mybir.dt.float32
U32 = mybir.dt.uint32
U8 = mybir.dt.uint8
FP8X4 = mybir.dt.float8_e4m3fn_x4

COPY = mybir.ActivationFunctionType.Copy
ALU = mybir.AluOpType

P = 128
PACK = 4
T, E, H = 1024, 512, 4
BANK = 512
CHUNKS = T // P
UNITS = H * CHUNKS
GROUP = P * PACK

FIRST = 12
SC = (2,)
LAG = 0
ORD = 4
SLOW = 24
VH = 26
W_EXTRA = (0,2)
WL = 1
WV = 3
GPSIMD_FROM = 4
GSPLIT = 1
X_ORDER = (0, 2, 4, 6, 1, 3, 5, 7)
U0 = 2
EARLY = 0
EARLY1 = 0
SINGLE = 16
SINGLE_END = 1
NEWEST = 0
NEWV = 0
RB = 11
GS = range(8,16)
WPOS = 1
R4 = 0
K7 = 0
AC = (12,13,14,16)
SAME = 0
SPLIT = 0
QF = 0
A5 = 0
PEO = 0
ACO = 3
MERGED = (1,2,3)
MH = 1
MQ = 1
SCM = 5
TQ = 24
SCK = 0
R3 = ()

SCALE = 1.0 / math.sqrt(T)

FLOPS = 2 * H * T * E * (2 * E + T)


def columns(i, width):
    return slice(i * width, (i + 1) * width)


def tile_multiheadattention_pa_kernel(tc, x, wq, wk, out):
    nc = tc.nc
    with ExitStack() as ctx:
        keep = ctx.enter_context(tc.tile_pool(name="keep", bufs=1))
        stage = ctx.enter_context(tc.tile_pool(name="stage", bufs=3))
        single = ctx.enter_context(tc.tile_pool(name="single", bufs=1))
        results = ctx.enter_context(tc.tile_pool(name="results", bufs=RB))
        psum = ctx.enter_context(tc.psum_pool(name="psum", bufs=8))
        ctx.enter_context(tc.manual_schedule())

        def load_weights(w, h, name):
            raw = keep.tile([P, PACK, E], BF16, name="%s_raw%d" % (name, h))
            nc.sync.dma_start(
                out=raw[:].rearrange("p (u e) o -> p u e o", u=2),
                in_=w[h].rearrange("(u p e) o -> p u e o", u=2, e=2),
            )
            return raw

        w_raw = [load_weights(wk, 0, "wk")]
        x_rows = x[0].rearrange("(p r) e -> p r e", r=CHUNKS)
        x_raw = []
        for a in range(CHUNKS // 2):
            piece = keep.tile([P, 2 * E], BF16, name="x_raw%d" % a)
            first_chunk = X_ORDER[2 * a]
            nc.sync.dma_start(
                out=piece[:].rearrange("p (r e) -> p r e", r=2),
                in_=x_rows[:, first_chunk : first_chunk + 3 : 2, :],
            )
            x_raw.append(piece)
        w_raw.append(load_weights(wq, 0, "wq"))
        for h in range(1, H):
            w_raw.append(load_weights(wk, h, "wk"))
            w_raw.append(load_weights(wq, h, "wq"))

        identity = keep.tile([P, P], F32, name="identity")
        make_identity(nc, identity[:])

        warm = keep.tile([P, 1], F32, name="warm")
        nc.vector.memset(warm[:], 0.0)
        nc.scalar.activation(out=warm[:], in_=warm[:], func=COPY)

        def mx_operand(name, width):
            codes = keep.tile([P, width], U32, name=name + "_codes", align_bytes=64)
            scales = keep.tile([P, width], U8, name=name + "_scales", align_bytes=64)
            return codes, scales

        def quantise(grouped, operand, where):
            codes, scales = operand
            nc.vector.quantize_mx(
                out=codes[:, where].bitcast(FP8X4), scales=scales[:, where], in_=grouped[:]
            )

        def mx_product(acc, stationary, stationary_columns, moving, moving_columns):
            nc.tensor.matmul_mx(
                out=acc,
                lhsT=stationary[0][:, stationary_columns].bitcast(FP8X4),
                lhsT_scale=stationary[1][:, stationary_columns],
                rhs=moving[0][:, moving_columns].bitcast(FP8X4),
                rhs_scale=moving[1][:, moving_columns],
                start=True,
                stop=True,
            )

        x_mx = mx_operand("x", T)
        w_mx = [mx_operand("w%d" % m, E) for m in range(2 * H)]
        q_mx = [mx_operand("q%d" % h, T) for h in range(H)]
        k_mx = [mx_operand("k%d" % h, T) for h in range(H)]

        x_grouped = {}

        def x_columns(r):
            return columns(X_ORDER.index(r), P)

        def transpose_x(a):
            words = x_raw[a][:].bitcast(F32)
            bank = psum.tile([P, 2, 2, P], F32, tag="bank", name="x_bank%d" % a)
            for r in range(2):
                for u in range(2):
                    nc.tensor.transpose(
                        bank[:, r, u, :], words[:, columns(2 * r + u, P)], identity[:]
                    )
            grouped = keep.tile([P, 2 * GROUP], BF16, name="x_grouped%d" % a, align_bytes=64)
            nc.scalar.copy(
                out=grouped[:].bitcast(F32).rearrange("p (r t u) -> p r t u", r=2, u=2),
                in_=bank[:].rearrange("p r u t -> p r t u"),
            )
            x_grouped[a] = grouped

        w_grouped = {}
        q_bank, q_grouped = {}, {}
        k_bank, k_grouped = {}, {}
        s_bank, result_of = {}, {}

        def regroup_whole(matrix):
            raw = w_raw[matrix]
            grouped = stage.tile(
                [P, 4 * GROUP], BF16, tag="w_whole", name="w_whole%d" % matrix, align_bytes=64, bufs=2
            )
            if matrix % 2 == 0:
                src = raw[:].rearrange("p t (n i) -> p n t i", i=4)
                dst = grouped[:].rearrange("p (n i t) -> p n t i", i=4, t=PACK)
            else:
                dst = grouped[:].rearrange("p (c m t) -> p m t c", c=PACK, t=PACK)
                src = raw[:].rearrange("p t (m c) -> p m t c", c=PACK)
            nc.vector.tensor_copy(out=dst, in_=src)
            w_grouped[2 * matrix] = grouped

        def regroup_weights(n):
            matrix, half = divmod(n, 2)
            if matrix in MERGED:
                if half == MH:
                    regroup_whole(matrix)
                return
            raw = w_raw[matrix]
            late = n in GS
            grouped = stage.tile(
                [P, 2 * GROUP], BF16, tag="w_late" if late and not SAME else "w_early", name="w_grouped%d" % n, align_bytes=64, bufs=WL if late and not SAME else WV
            )
            if matrix % 2 == 0:
                src = raw[:, :, columns(half, 2 * P)]
                if late:
                    src = src.rearrange("p t n -> p n t")
                    dst = grouped[:].rearrange("p (n t) -> p n t", t=PACK)
                else:
                    src = src.rearrange("p t (n i) -> p n t i", i=4)
                    dst = grouped[:].rearrange("p (n i t) -> p n t i", i=4, t=PACK)
            else:
                dst = grouped[:].rearrange("p (c m t) -> p c m t", c=2, t=PACK)
                src = raw[:].rearrange("p t (m c) -> p c m t", c=PACK)[:, 2 * half : 2 * half + 2]
            if late:
                for s in range(GSPLIT):
                    if matrix % 2 == 0:
                        part = columns(s, 2 * P // GSPLIT)
                        d2, s2 = dst[:, part], src[:, part]
                    elif GSPLIT == 4:
                        part = columns(s % 2, P // 2)
                        d2, s2 = dst[:, s // 2, part], src[:, s // 2, part]
                    else:
                        part = columns(s, 2 // GSPLIT)
                        d2, s2 = dst[:, part], src[:, part]
                    nc.gpsimd.tensor_scalar(
                        out=d2, in0=s2, scalar1=1.0, scalar2=0.0, op0=ALU.mult, op1=ALU.add
                    )
            else:
                nc.vector.tensor_copy(out=dst, in_=src)
            w_grouped[n] = grouped

        def quantise_weights(n):
            matrix, half = divmod(n, 2)
            if matrix in MERGED:
                if half == MQ:
                    quantise(w_grouped[2 * matrix], w_mx[matrix], slice(0, E))
                return
            quantise(w_grouped[n], w_mx[matrix], columns(half, 2 * P))

        def empty_projection(copy_out, bank, grouped, place):
            copy_out(
                out=grouped[:, columns(place, GROUP)].rearrange("p (n c) -> p n c", c=PACK),
                in_=bank[:].rearrange("p c n -> p n c"),
            )

        def project_q(m):
            h, r = divmod(m, CHUNKS)
            bank = psum.tile([P, PACK, P], F32, tag="bank", name="q_bank%d" % m)
            for c in range(PACK):
                mx_product(bank[:, c, :], w_mx[2 * h + 1], columns(c, P), x_mx, x_columns(r))
            q_bank[m] = bank

        def empty_q(m, copy_out):
            if m // 2 not in q_grouped:
                q_grouped[m // 2] = stage.tile(
                    [P, 2 * GROUP], BF16, tag="q_grouped", name="q_grouped%d" % m, align_bytes=64
                )
            empty_projection(copy_out, q_bank[m], q_grouped[m // 2], m % 2)

        def quantise_q(pair):
            h, j = divmod(pair, CHUNKS // 2)
            quantise(q_grouped[pair], q_mx[h], columns(j, 2 * P))

        def project_k(n):
            h, j_chunk = divmod(n, CHUNKS)
            jh, b = divmod(j_chunk, PACK)
            bank = psum.tile([P, PACK, P], F32, tag="bank", name="k_bank%d" % n)
            for c in range(PACK):
                mx_product(bank[:, c, :], x_mx, x_columns(2 * c + jh), w_mx[2 * h], columns(b, P))
            k_bank[n] = bank

        def empty_k(n, copy_out):
            if n // PACK not in k_grouped:
                k_grouped[n // PACK] = stage.tile(
                    [P, PACK * GROUP], BF16, tag="k_grouped", name="k_grouped%d" % n, align_bytes=64
                )
            empty_projection(copy_out, k_bank[n], k_grouped[n // PACK], n % PACK)

        def quantise_k(half):
            quantise(k_grouped[half], k_mx[half // 2], columns(half % 2, BANK))

        def place(u):
            h, rest = divmod(u, CHUNKS)
            if ORD == 2:
                return h, [(rest, 0), (rest, 1)]
            a, rest = divmod(rest, 4)
            jh, b = divmod(rest, 2)
            if a == 1 and ORD == 4:
                b, jh = jh, b
            j = 2 * a + b
            return h, [(2 * j, jh), (2 * j + 1, jh)]

        def multiply_scores(u, which=(0, 1)):
            h, banks = place(u)
            for i in which:
                r, jh = banks[i]
                bank = psum.tile([P, BANK], F32, tag="bank", name="s_bank%d_%d" % (u, i))
                mx_product(bank[:], q_mx[h], columns(r, P), k_mx[h], columns(jh, BANK))
                s_bank[(u, i)] = bank

        def empty_scores(u, i, on_vector):
            rows = result_of[u // 2][:, 2 * (u % 2) + i, :]
            if on_vector:
                nc.vector.tensor_scalar_mul(out=rows, in0=s_bank[(u, i)][:], scalar1=SCALE)
            else:
                nc.scalar.activation(out=rows, in_=s_bank[(u, i)][:], func=COPY, scale=SCALE)

        out_rows = [out[h, 0].rearrange("(p r) j -> p r j", r=CHUNKS) for h in range(H)]

        def store_unit(u):
            h, banks = place(u)
            r, jh = banks[0]
            pair = result_of[u // 2]
            if u // 2 < SINGLE or u // 2 >= UNITS // 2 - SINGLE_END:
                nc.sync.dma_start(
                    out=out_rows[h][:, r : r + 2, columns(jh, BANK)], in_=pair[:, columns(u % 2, 2), :]
                )
            elif u % 2 == 1:
                nc.sync.dma_start(out=out_rows[h][:, r - 2 : r + 2, columns(jh, BANK)], in_=pair[:])

        def exists(i):
            return 0 <= i < UNITS

        def need(kind, n):
            j = n % CHUNKS // 2
            if ORD == 2:
                return CHUNKS * (n // CHUNKS) + (0 if kind == 0 else 2 * j)
            if kind == 0:
                return 0 if n < CHUNKS else CHUNKS * (n // CHUNKS) + 2 * (n % CHUNKS // PACK)
            return CHUNKS * (n // CHUNKS) + 4 * (j // 2) + j % 2 * (2 if j // 2 and ORD == 4 else 1)
        order = sorted([(need(k, n), k, n) for k in (0, 1) for n in range(UNITS)])
        def project(i):
            kind, n = order[i][1:]
            if kind == 0:
                project_k(n)
            else:
                project_q(n)

        quants = []
        copied = {}

        def empty(i, copy_out):
            kind, n = order[i][1:]
            if kind == 0:
                empty_k(n, copy_out)
                group = (0, n // PACK)
            else:
                empty_q(n, copy_out)
                group = (1, n // 2)
            copied[group] = copied.get(group, 0) + 1
            if copied[group] == (PACK if kind == 0 else 2):
                quants.append(group)

        def quantise_group(group):
            if group[0] == 0:
                quantise_k(group[1])
            else:
                quantise_q(group[1])

        on_scalar, on_vector = nc.scalar.copy, nc.vector.tensor_copy
        regroup_weights(0)
        regroup_weights(1)
        for a in range(4):
            transpose_x(a)
        quantise_weights(0)
        quantise_weights(1)
        for a in range(2):
            quantise(x_grouped[a], x_mx, columns(a, 2 * P))
        for i in range(4):
            project(i)
        for a in range(2, 4):
            quantise(x_grouped[a], x_mx, columns(a, 2 * P))
        regroup_weights(2)
        regroup_weights(3)
        for i in range(4, 8):
            project(i)
        for i in range(6 - A5):
            empty(i, on_scalar)
        quantise_weights(3)
        quantise_weights(2)
        quantise_group(quants.pop(0))
        for i in range(8, FIRST):
            project(i)
        empty(8, on_vector)
        empty(9, on_scalar)
        if A5:
            empty(5, on_scalar)
        if QF == 2:
            quantise_group(quants.pop(0))
        empty(11, on_scalar)
        empty(10, on_vector)
        if QF == 1:
            quantise_group(quants.pop(0))
        empty(6, on_scalar)
        if R4 == 0:
            regroup_weights(4)
        if not QF:
            quantise_group(quants.pop(0))
        quantise_group(quants.pop(0))
        if R4 == 1:
            regroup_weights(4)
        if K7 == 0:
            empty(7, on_scalar)
        elif K7 == 1:
            empty(7, on_vector)
        if ORD == 2:
            quantise_group(quants.pop(0))
        regroup_weights(5)
        quantise_weights(4)
        next_w = 5
        regrouped = 6
        while regrouped < next_w + (WL if regrouped in GS and not SAME else WV):
            regroup_weights(regrouped)
            regrouped += 1
        done = FIRST
        for u in range(UNITS):
            total = len(order)
            first = done
            done = min(total, done + (1 if u >= SLOW or u < EARLY1 else 3 if u in R3 else 2))
            busy = first < total
            vhelp = not busy or u >= VH
            if PEO == 0:
                multiply_scores(u)
            if PEO == 2 and done > first:
                multiply_scores(u, (0,))
                project(first)
                multiply_scores(u, (1,))
                for i in range(first + 1, done):
                    project(i)
            elif PEO == 2:
                multiply_scores(u)
            else:
                for i in range(first, done):
                    project(i)
            if PEO == 1:
                multiply_scores(u)
            if u % 2 == 0:
                result_of[u // 2] = results.tile([P, 4, BANK], F32, tag="result", name="result%d" % u)
            s_order = ((1, 0) if NEWEST else (0, 1))
            early_copy = [i for i in range(first, done) if (i in AC if i < 20 else (i % SCM in SC if SCK == 0 else order[i][1] == SCK - 1 and order[i][2] % SCM in SC))]
            if ACO == 1:
                for i in early_copy:
                    empty(i, on_scalar)
            empty_scores(u, s_order[0], on_vector=False)
            if ACO == 2 or ACO == 3 and u >= 2:
                for i in early_copy:
                    empty(i, on_scalar)
            empty_scores(u, s_order[1], on_vector=vhelp)
            if ACO == 0 or ACO == 3 and u < 2:
                for i in early_copy:
                    empty(i, on_scalar)
            if u % 2 == 0 or u < U0:
                ready = quants[:]
            if u < U0 and EARLY:
                for g in ready:
                    quantise_group(g)
                    quants.remove(g)
                ready = []
            for i in (range(done - 1, first - 1, -1) if NEWV else range(first, done)):
                if i < total:
                    if i not in early_copy:
                        empty(i, on_vector)
                    if u % 2 == 1 and i == (first if NEWV else done - 1):
                        ready = quants[:]
            if u % 2 == 1 or not busy or u < U0 or u >= TQ:
                due = ready if busy and u < TQ else quants[:]
                w_now = (u % 2 == 1 or u in W_EXTRA) and next_w < 4 * H
                for x, g in enumerate(due):
                    if WPOS and w_now and x == len(due) - 1:
                        quantise_weights(next_w)
                    quantise_group(g)
                    quants.remove(g)
                w_done = WPOS and w_now and len(due) > 0
            else:
                w_done = False
            if u % 2 == 1 or u in W_EXTRA:
                if next_w < 4 * H:
                    if not w_done:
                        quantise_weights(next_w)
                    next_w += 1
                    while regrouped < 4 * H and regrouped < next_w + (WL if regrouped in GS and not SAME else WV) :
                        regroup_weights(regrouped)
                        regrouped += 1
            store_unit(u)
